import numpy as np
import ml_dtypes


def mxq(x, axis, fmt="e4m3"):
    dtype, down = {"e4m3": (ml_dtypes.float8_e4m3fn, 7), "e5m2": (ml_dtypes.float8_e5m2, 14)}[fmt]
    v = np.moveaxis(np.asarray(x, np.float32).astype(ml_dtypes.bfloat16).astype(np.float64), axis, -1)
    blocks = v.reshape(v.shape[:-1] + (-1, 32))
    amax = np.abs(blocks).max(-1, keepdims=True)
    byte = np.maximum(np.where(amax > 0, np.frexp(amax)[1] - 1 + 127, 0) - down, 1)
    scale = np.exp2(byte - 127.0)
    codes = (blocks / scale).astype(np.float32).astype(dtype).astype(np.float64)
    return np.moveaxis((codes * scale).reshape(v.shape), -1, axis)


WIDE = False


def mx_kscale(k):
    if not WIDE:
        return np.ones(k)
    levels = np.array([10, -10, 5, -5, 0])
    a = np.random.permutation(np.resize(levels, k // 512 * 4)).reshape(k // 512, 4)
    idx = np.arange(k)
    return np.exp2(a[idx // 512, idx % 128 // 32])


BF16 = ml_dtypes.bfloat16


def bf(x):
    return np.asarray(x, np.float32).astype(BF16)


def f64(x):
    return np.asarray(x).astype(np.float64)


E2M1 = np.array([0.0, 0.5, 1.0, 1.5, 2.0, 3.0, 4.0, 6.0, -0.0, -0.5, -1.0, -1.5, -2.0, -3.0, -4.0, -6.0])


def pack_weight(w, fmt):
    k, n = w.shape
    w = f64(bf(w)).reshape(k // 32, 32, n)
    amax = np.abs(w).max(1)
    if fmt == "e4m3":
        byte = np.frexp(amax)[1] - 1 + 127 - 7
    else:
        mant, ex = np.frexp(amax / 6.0)
        byte = np.where(mant > 0.5, ex, ex - 1) + 127
    byte = np.clip(np.where(amax > 0, byte, 1), 1, 254)
    scaled = (w * np.exp2(127.0 - byte)[:, None, :]).reshape(k, n).astype(np.float32)
    by_word = np.ascontiguousarray(scaled.reshape(k // 512, 128, 4, n).transpose(0, 1, 3, 2))
    if fmt == "e4m3":
        words = by_word.astype(ml_dtypes.float8_e4m3fn).view(np.uint8)
    else:
        c = by_word.astype(ml_dtypes.float4_e2m1fn).view(np.uint8) & 0xF
        words = c[..., 0::2] | (c[..., 1::2] << 4)
    return np.ascontiguousarray(words), np.ascontiguousarray(byte.astype(np.uint8).reshape(k // 512, 16, n))


def unpack_weight(words, scales, fmt):
    g, p, n, _ = words.shape
    if fmt == "e4m3":
        vals = np.ascontiguousarray(words).view(ml_dtypes.float8_e4m3fn).astype(np.float64)
    else:
        nib = np.empty((g, p, n, 4), np.uint8)
        nib[..., 0::2] = words & 0xF
        nib[..., 1::2] = words >> 4
        vals = E2M1[nib]
    vals = vals * np.repeat(np.exp2(scales.astype(np.float64) - 127.0), 8, axis=1)[..., None]
    return vals.transpose(0, 1, 3, 2).reshape(g * 512, n)


B, S, T, E, D, H = 1, 512, 512, 8192, 1024, 8
DK = D // H


def rope_tables(n):
    m = np.arange(n, dtype=np.float64)[:, None]
    i = np.repeat(np.arange(DK // 2, dtype=np.float64), 2)[None, :]
    ang = m * np.exp(-(2.0 * np.log(1e4) / DK) * i)
    return np.cos(ang), np.sin(ang)


def rotate_pairs(x):
    return np.stack([-x[..., 1::2], x[..., 0::2]], axis=-1).reshape(x.shape)


def setup_inputs():
    s = mx_kscale(E)
    q_rot = bf(np.random.standard_normal((B, H, T, DK)) * 1.2)
    k_rot = bf(np.random.standard_normal((B, H, S, DK)) * 1.2)
    values = bf(np.random.standard_normal((B, S, E)) * s)
    wv_words, wv_scales = pack_weight(np.random.standard_normal((E, D)) * 3.0 / np.sqrt(E) / s[:, None], "e4m3")
    bv = bf(np.random.standard_normal(D) * 0.8)
    return {"q_rot": q_rot,
            "k_rot": k_rot,
            "values": values,
            "wv_words": wv_words,
            "wv_scales": wv_scales,
            "bv": bv}


def reference(q_rot, k_rot, values, wv_words, wv_scales, bv):
    v = (mxq(f64(values), 2, "e4m3") @ unpack_weight(wv_words, wv_scales, "e4m3")) + f64(bv)
    v = v.reshape(B, S, H, DK).transpose(0, 2, 1, 3)
    r1, r2 = rope_tables(S)
    v = v * r1 + rotate_pairs(v) * r2
    sc = (f64(q_rot) @ f64(k_rot).transpose(0, 1, 3, 2)) * DK ** -0.5
    e = np.exp(sc - sc.max(-1, keepdims=True))
    y = (mxq(e, 3, "e4m3") @ mxq(v, 2, "e4m3")) / e.sum(-1, keepdims=True)
    return y.transpose(0, 2, 1, 3).reshape(B, T, D)

@@ -1,0 +1,395 @@
+import math
+from contextlib import ExitStack
+
+import concourse.mybir as mybir
+from concourse.masks import make_identity
+
+F32 = mybir.dt.float32
+BF16 = mybir.dt.bfloat16
+I32 = mybir.dt.int32
+U32 = mybir.dt.uint32
+U8 = mybir.dt.uint8
+FP8X4 = mybir.dt.float8_e4m3fn_x4
+ALU = mybir.AluOpType
+ACT = mybir.ActivationFunctionType
+AX = mybir.AxisListType
+
+P = 128
+PACK = 4
+K_PASS = P * PACK
+SEQ = 512
+ROWS = SEQ // P
+EMB = 8192
+GROUPS = EMB // K_PASS
+WIDTH = 1024
+HEADS = 8
+DK = 128
+HALF = DK // 2
+SCALE = DK ** -0.5
+
+CHUNK_GROUPS = 2
+CHUNK_K = CHUNK_GROUPS * K_PASS
+CHUNKS = GROUPS // CHUNK_GROUPS
+X_BUFS = 6
+
+ROUND_HEADS = 2
+ROUND_COLS = ROUND_HEADS * DK
+ROUNDS = HEADS // ROUND_HEADS
+
+BUNCH = 2
+BUNCHES = HEADS * ROWS // BUNCH
+HEAD_BUNCHES = ROWS // BUNCH
+PLAIN_BUNCHES = 6
+
+TWO_PI_PARTS = (6.28125, 0.0019353071693331003, 1.0253131677018246e-11)
+SIN_BOUND = 3.1415925
+
+FLOPS = 2 * SEQ * EMB * WIDTH + 2 * 2 * HEADS * SEQ * SEQ * DK
+
+
+def tile_multiheadedattention_pb_k_kernel(tc, q_rot, k_rot, values, wv_words, wv_scales, bv, out):
+    nc = tc.nc
+
+    x_view = values.rearrange("o (p r) k -> (o p) r k", r=ROWS)
+    q_view = q_rot.rearrange("o h (p a) d -> p (o h) (a d)", a=ROWS)
+    k_view = k_rot.rearrange("o h (p r) d -> p (o h) (r d)", r=ROWS)
+    w_view = wv_words.rearrange("g p n t -> p g (n t)").bitcast(I32)
+    s_view = wv_scales.bitcast(I32)
+    out_view = out.rearrange("o (p a) n -> (o p) a n", a=ROWS)
+
+    with ExitStack() as ctx:
+        ctx.enter_context(tc.manual_schedule())
+        keep = ctx.enter_context(tc.tile_pool(name="keep", bufs=1))
+        e_pool = ctx.enter_context(tc.tile_pool(name="e_pool", bufs=2 * BUNCH))
+        eg_pool = ctx.enter_context(tc.tile_pool(name="eg_pool", bufs=2))
+        small = ctx.enter_context(tc.tile_pool(name="small", bufs=2 * BUNCH))
+        ps_sc = ctx.enter_context(tc.psum_pool(name="ps_sc", bufs=BUNCH))
+        ps_tp = ctx.enter_context(tc.psum_pool(name="ps_tp", bufs=2))
+
+        ident_bf = keep.tile([P, P], BF16)
+        ident_f32 = keep.tile([P, P], F32)
+        x_codes = keep.tile([P, GROUPS, SEQ], U32, align_bytes=64)
+        x_scales = keep.tile([P, GROUPS, SEQ], U8, align_bytes=64)
+        w_planes = keep.tile([P, GROUPS // 4, WIDTH], U8, align_bytes=64)
+        qk_raw = keep.tile([P, 2, HEADS, SEQ], BF16)
+        qk_t = keep.tile([P, HEADS, 2 * ROWS, P], BF16)
+        e_codes = keep.tile([P, HEADS, SEQ], U32, align_bytes=64)
+        e_scales = keep.tile([P, HEADS, SEQ], U8, align_bytes=64)
+        v_codes = keep.tile([P, WIDTH], U32, align_bytes=64)
+        v_scales = keep.tile([P, WIDTH], U8, align_bytes=64)
+        sin_t = keep.tile([P, ROWS, HALF], F32)
+        cos_t = keep.tile([P, ROWS, HALF], F32)
+        bias_pl = keep.tile([P, 2, WIDTH // 2], F32)
+        rowsum = keep.tile([P, ROWS, HEADS], F32)
+        rinv = keep.tile([P, ROWS, HEADS], F32)
+        w_codes = [
+            keep.tile([P, GROUPS, ROUND_COLS], U32, align_bytes=64, name="w_codes_%d" % rnd) for rnd in range(2)
+        ]
+
+        e_tiles = {}
+        e_groups = {}
+
+        def load_qk(pair):
+            heads = slice(2 * pair, 2 * pair + 2)
+            nc.sync.dma_start(out=qk_raw[:, 1, heads, :], in_=k_view[:, heads, :])
+            nc.sync.dma_start(out=qk_raw[:, 0, heads, :], in_=q_view[:, heads, :])
+
+        def load_w(rnd, tile_):
+            cols = slice(rnd * ROUND_COLS, (rnd + 1) * ROUND_COLS)
+            for half in range(2):
+                gs = slice(half * GROUPS // 2, (half + 1) * GROUPS // 2)
+                nc.sync.dma_start(out=tile_[:, gs, :].bitcast(I32), in_=w_view[:, gs, cols])
+
+        def transpose_qk(h):
+            tp = ps_tp.tile([P, 2 * ROWS, P], BF16, tag="tp")
+            for which in range(2):
+                for row in range(ROWS):
+                    nc.tensor.transpose(
+                        tp[:, which * ROWS + row, :], qk_raw[:, which, h, row * DK : (row + 1) * DK], ident_bf[:]
+                    )
+            nc.scalar.copy(out=qk_t[:, h, :, :], in_=tp[:])
+
+        def scores(b):
+            h = b // HEAD_BUNCHES
+            e_tiles[b] = []
+            for i in range(BUNCH):
+                a = (b % HEAD_BUNCHES) * BUNCH + i
+                sc = ps_sc.tile([P, SEQ], F32, tag="sc")
+                nc.tensor.matmul(
+                    out=sc[:],
+                    lhsT=qk_t[:, h, a, :],
+                    rhs=qk_t[:, h, ROWS : 2 * ROWS, :].rearrange("d r s -> d (r s)"),
+                    start=True,
+                    stop=True,
+                )
+                top = small.tile([P, 1], F32, tag="top")
+                nc.vector.reduce_max(out=top[:], in_=sc[:], axis=AX.X)
+                shift = small.tile([P, 1], F32, tag="shift")
+                nc.vector.tensor_scalar_mul(out=shift[:], in0=top[:], scalar1=-SCALE)
+                e_sb = e_pool.tile([P, SEQ], BF16, tag="e_sb")
+                nc.scalar.activation(
+                    out=e_sb[:],
+                    in_=sc[:],
+                    func=ACT.Exp,
+                    bias=shift[:],
+                    scale=SCALE,
+                    accum_out=rowsum[:, a, h : h + 1],
+                )
+                e_tiles[b].append(e_sb)
+
+        def transpose_e(b):
+            h = b // HEAD_BUNCHES
+            first = (b % HEAD_BUNCHES) * BUNCH
+            if first == 0:
+                e_groups[h] = eg_pool.tile([P, ROWS, P, PACK], BF16, align_bytes=64, tag="e_grp", name="e_grp")
+            tp = ps_tp.tile([P, BUNCH * ROWS, P], BF16, tag="tp")
+            for i in range(BUNCH):
+                for r in range(ROWS):
+                    nc.tensor.transpose(tp[:, i * ROWS + r, :], e_tiles[b][i][:, r * P : (r + 1) * P], ident_bf[:])
+            nc.scalar.copy(
+                out=e_groups[h][:, first : first + BUNCH, :, :],
+                in_=tp[:].rearrange("p (a r) t -> p a t r", r=ROWS),
+            )
+
+        def quantise_e(h):
+            nc.vector.quantize_mx(
+                out=e_codes[:, h, :].bitcast(FP8X4),
+                scales=e_scales[:, h, :],
+                in_=e_groups[h][:].rearrange("p a t r -> p (a t r)"),
+            )
+
+        def attention_bunch(b):
+            if b >= 1:
+                transpose_e(b - 1)
+            if b % HEAD_BUNCHES == HEAD_BUNCHES - 1 and b + 1 < BUNCHES:
+                transpose_qk((b + 1) // HEAD_BUNCHES)
+            if b < BUNCHES:
+                scores(b)
+            if b >= 1 and b % HEAD_BUNCHES == 0:
+                quantise_e(b // HEAD_BUNCHES - 1)
+
+        with ExitStack() as plain:
+            x_pool = plain.enter_context(tc.tile_pool(name="x_pool", bufs=X_BUFS))
+            grp_pool = plain.enter_context(tc.tile_pool(name="grp_pool", bufs=3))
+            tab = plain.enter_context(tc.tile_pool(name="tab", bufs=1))
+            ps_xt = plain.enter_context(tc.psum_pool(name="ps_xt", bufs=4))
+
+            def load_chunk(c):
+                x_raw = x_pool.tile([P, ROWS, CHUNK_K], BF16, tag="x_raw")
+                nc.sync.dma_start(out=x_raw[:], in_=x_view[:, :, c * CHUNK_K : (c + 1) * CHUNK_K])
+                return x_raw
+
+            x_tiles = []
+            load_qk(0)
+            for c in range(4):
+                x_tiles.append(load_chunk(c))
+            load_qk(1)
+            for c in range(4, X_BUFS):
+                x_tiles.append(load_chunk(c))
+
+            make_identity(nc, ident_bf[:])
+            make_identity(nc, ident_f32[:])
+            nc.vector.memset(w_planes[:].bitcast(I32), 0)
+
+            idx_i = tab.tile([P, HALF], I32)
+            nc.gpsimd.iota(idx_i[:], pattern=[[1, HALF]], base=0, channel_multiplier=0)
+            pos_i = tab.tile([P, ROWS], I32)
+            nc.gpsimd.iota(pos_i[:], pattern=[[1, ROWS]], base=0, channel_multiplier=ROWS)
+            idx_f = tab.tile([P, HALF], F32)
+            nc.vector.tensor_copy(out=idx_f[:], in_=idx_i[:])
+            pos_f = tab.tile([P, ROWS], F32)
+            nc.vector.tensor_copy(out=pos_f[:], in_=pos_i[:])
+            freq = tab.tile([P, HALF], F32)
+            nc.scalar.activation(out=freq[:], in_=idx_f[:], func=ACT.Exp, scale=-2.0 * math.log(10000.0) / DK)
+            angle = tab.tile([P, ROWS, HALF], F32)
+            nc.vector.tensor_tensor(
+                out=angle[:],
+                in0=freq[:].unsqueeze(1).to_broadcast([P, ROWS, HALF]),
+                in1=pos_f[:].unsqueeze(2).to_broadcast([P, ROWS, HALF]),
+                op=ALU.mult,
+            )
+            turns_i = tab.tile([P, ROWS, HALF], I32)
+            nc.vector.tensor_scalar_mul(out=turns_i[:], in0=angle[:], scalar1=0.5 / math.pi)
+            cut = tab.tile([P, ROWS, HALF], F32)
+            nc.vector.tensor_copy(out=cut[:], in_=turns_i[:])
+            left = tab.tile([P, ROWS, HALF], F32)
+            nc.vector.scalar_tensor_tensor(
+                out=left[:], in0=cut[:], scalar=-2.0 * math.pi, in1=angle[:], op0=ALU.mult, op1=ALU.add
+            )
+            turns = tab.tile([P, ROWS, HALF], F32)
+            nc.vector.scalar_tensor_tensor(
+                out=turns[:], in0=left[:], scalar=math.pi, in1=cut[:], op0=ALU.is_gt, op1=ALU.add
+            )
+            for part in TWO_PI_PARTS:
+                nc.vector.scalar_tensor_tensor(
+                    out=angle[:], in0=turns[:], scalar=-part, in1=angle[:], op0=ALU.mult, op1=ALU.add
+                )
+            nc.vector.tensor_scalar(
+                out=angle[:], in0=angle[:], scalar1=-SIN_BOUND, scalar2=SIN_BOUND, op0=ALU.max, op1=ALU.min
+            )
+            nc.scalar.activation(out=sin_t[:], in_=angle[:], func=ACT.Sin)
+            half_sin = tab.tile([P, ROWS, HALF], F32)
+            nc.scalar.activation(out=half_sin[:], in_=angle[:], func=ACT.Sin, scale=0.5)
+            nc.gpsimd.tensor_tensor(out=half_sin[:], in0=half_sin[:], in1=half_sin[:], op=ALU.mult)
+            nc.gpsimd.tensor_scalar(out=cos_t[:], in0=half_sin[:], scalar1=-2.0, scalar2=1.0, op0=ALU.mult, op1=ALU.add)
+
+            b_raw = tab.tile([P, WIDTH], BF16)
+
+            def load_rest():
+                for a in range(GROUPS // 4):
+                    for quad in range(4):
+                        nc.sync.dma_start(
+                            out=w_planes[32 * quad : 32 * quad + 16, a, :].bitcast(I32),
+                            in_=s_view[4 * a : 4 * a + 4, 4 * quad : 4 * quad + 4, :],
+                        )
+                load_w(0, w_codes[0])
+                nc.sync.dma_start(out=b_raw[:], in_=bv.partition_broadcast(P))
+                nc.gpsimd.tensor_copy(out=bias_pl[:], in_=b_raw[:].rearrange("p (x two) -> p two x", two=2))
+                load_qk(2)
+                load_w(1, w_codes[1])
+                load_qk(3)
+
+            def transpose_group(g):
+                x_raw = x_tiles[g // CHUNK_GROUPS]
+                first_k = (g % CHUNK_GROUPS) * K_PASS
+                grouped = grp_pool.tile([P, ROWS, P, PACK], BF16, align_bytes=64, tag="grouped")
+                for half in range(2):
+                    xt = ps_xt.tile([P, 2, 2, P], F32, tag="xt")
+                    for r2 in range(2):
+                        words = x_raw[:, 2 * half + r2, first_k : first_k + K_PASS].bitcast(F32)
+                        for u in range(2):
+                            nc.tensor.transpose(xt[:, r2, u, :], words[:, u : K_PASS // 2 : 2], ident_f32[:])
+                    dst = grouped[:, 2 * half : 2 * half + 2, :, :].bitcast(F32)
+                    src = xt[:].rearrange("p r u s -> p r s u")
+                    if half == 0:
+                        nc.vector.tensor_copy(out=dst, in_=src)
+                    else:
+                        nc.scalar.copy(out=dst, in_=src)
+                return grouped
+
+            def quantise_group(g, grouped):
+                nc.vector.quantize_mx(
+                    out=x_codes[:, g, :].bitcast(FP8X4),
+                    scales=x_scales[:, g, :],
+                    in_=grouped[:].rearrange("p r s j -> p (r s j)"),
+                )
+
+            transpose_qk(0)
+            waiting = None
+            for g in range(GROUPS):
+                grouped = transpose_group(g)
+                if waiting is not None:
+                    quantise_group(g - 1, waiting)
+                waiting = grouped
+                next_chunk = g // CHUNK_GROUPS + X_BUFS
+                if g % CHUNK_GROUPS == CHUNK_GROUPS - 1 and next_chunk < CHUNKS:
+                    x_tiles.append(load_chunk(next_chunk))
+                    if next_chunk == CHUNKS - 1:
+                        load_rest()
+                for b in range(g * PLAIN_BUNCHES // GROUPS, (g + 1) * PLAIN_BUNCHES // GROUPS):
+                    attention_bunch(b)
+            quantise_group(GROUPS - 1, waiting)
+
+        with ExitStack() as mx:
+            late = mx.enter_context(tc.tile_pool(name="late", bufs=1, reuse_waits="tile"))
+            rope = mx.enter_context(tc.tile_pool(name="rope", bufs=3, reuse_waits="tile"))
+            v_pool = mx.enter_context(tc.tile_pool(name="v_pool", bufs=2, reuse_waits="tile"))
+            ps_z = mx.enter_context(tc.psum_pool(name="ps_z", bufs=2, reuse_waits="tile"))
+            ps_y = mx.enter_context(tc.psum_pool(name="ps_y", bufs=2, reuse_waits="tile"))
+
+            for rnd in range(2, ROUNDS):
+                w_codes.append(late.tile([P, GROUPS, ROUND_COLS], U32, align_bytes=64, name="w_codes_%d" % rnd))
+                load_w(rnd, w_codes[rnd])
+
+            v_rows = {}
+
+            def project(rnd, r):
+                z = ps_z.tile([P, ROUND_COLS], F32, tag="z")
+                rows = slice(r * P, (r + 1) * P)
+                cols = slice(rnd * ROUND_COLS, (rnd + 1) * ROUND_COLS)
+                for g in range(GROUPS):
+                    nc.tensor.matmul_mx(
+                        out=z[:],
+                        lhsT=x_codes[:, g, rows].bitcast(FP8X4),
+                        lhsT_scale=x_scales[:, g, rows],
+                        rhs=w_codes[rnd][:, g, :].bitcast(FP8X4),
+                        rhs_scale=w_planes[4 * (g % 4) : P, g // 4, cols],
+                        start=(g == 0),
+                        stop=(g == GROUPS - 1),
+                    )
+                return z
+
+            def rotate(rnd, r, z):
+                if r == 0:
+                    v_rows[rnd] = v_pool.tile([P, ROWS, 2, ROUND_COLS // 2], BF16, tag="v_rows", name="v_rows")
+                eng = nc.vector if rnd == ROUNDS - 1 else nc.gpsimd
+                xs = slice(rnd * ROUND_COLS // 2, (rnd + 1) * ROUND_COLS // 2)
+                zb = rope.tile([P, 2, ROUND_COLS // 2], F32, tag="zb")
+                nc.vector.tensor_tensor(
+                    out=zb[:], in0=z[:].rearrange("p (x two) -> p two x", two=2), in1=bias_pl[:, :, xs], op=ALU.add
+                )
+                by_cos = rope.tile([P, 2, ROUND_COLS // 2], F32, tag="by_cos")
+                by_sin = rope.tile([P, 2, ROUND_COLS // 2], F32, tag="by_sin")
+                for table, prod in ((cos_t, by_cos), (sin_t, by_sin)):
+                    eng.tensor_tensor(
+                        out=prod[:].rearrange("p two (h i) -> p (two h) i", i=HALF),
+                        in0=zb[:].rearrange("p two (h i) -> p (two h) i", i=HALF),
+                        in1=table[:, r, :].unsqueeze(1).to_broadcast([P, 2 * ROUND_HEADS, HALF]),
+                        op=ALU.mult,
+                    )
+                eng.tensor_tensor(out=v_rows[rnd][:, r, 0, :], in0=by_cos[:, 0, :], in1=by_sin[:, 1, :], op=ALU.subtract)
+                eng.tensor_tensor(out=v_rows[rnd][:, r, 1, :], in0=by_cos[:, 1, :], in1=by_sin[:, 0, :], op=ALU.add)
+
+            def quantise_v(rnd):
+                cols = slice(rnd * ROUND_COLS, (rnd + 1) * ROUND_COLS)
+                v_grp = v_pool.tile([P, ROUND_COLS, PACK], BF16, align_bytes=64, tag="v_grp")
+                nc.vector.tensor_copy(
+                    out=v_grp[:].rearrange("p (x two) r -> p x two r", two=2),
+                    in_=v_rows[rnd][:].rearrange("p r two x -> p x two r"),
+                )
+                nc.vector.quantize_mx(
+                    out=v_codes[:, cols].bitcast(FP8X4),
+                    scales=v_scales[:, cols],
+                    in_=v_grp[:].rearrange("p n r -> p (n r)"),
+                )
+
+            def attend(rnd):
+                heads = slice(rnd * ROUND_HEADS, (rnd + 1) * ROUND_HEADS)
+                nc.vector.reciprocal(out=rinv[:, :, heads], in_=rowsum[:, :, heads])
+                y_sb = v_pool.tile([P, ROWS, ROUND_COLS], F32, tag="y_sb")
+                for pair in range(ROWS // 2):
+                    y = ps_y.tile([P, 2, ROUND_HEADS, DK], F32, tag="y")
+                    for a2 in range(2):
+                        a = 2 * pair + a2
+                        for h2 in range(ROUND_HEADS):
+                            h = rnd * ROUND_HEADS + h2
+                            nc.tensor.matmul_mx(
+                                out=y[:, a2, h2, :],
+                                lhsT=e_codes[:, h, a * P : (a + 1) * P].bitcast(FP8X4),
+                                lhsT_scale=e_scales[:, h, a * P : (a + 1) * P],
+                                rhs=v_codes[:, h * DK : (h + 1) * DK].bitcast(FP8X4),
+                                rhs_scale=v_scales[:, h * DK : (h + 1) * DK],
+                                start=True,
+                                stop=True,
+                            )
+                    nc.vector.tensor_tensor(
+                        out=y_sb[:, 2 * pair : 2 * pair + 2, :].rearrange("p a (h j) -> p a h j", j=DK),
+                        in0=y[:],
+                        in1=rinv[:, 2 * pair : 2 * pair + 2, heads].unsqueeze(3).to_broadcast([P, 2, ROUND_HEADS, DK]),
+                        op=ALU.mult,
+                    )
+                nc.sync.dma_start(out=out_view[:, :, rnd * ROUND_COLS : (rnd + 1) * ROUND_COLS], in_=y_sb[:])
+
+            for rnd in range(ROUNDS):
+                for r in range(ROWS):
+                    z = project(rnd, r)
+                    rotate(rnd, r, z)
+                    if rnd >= 1 and r == 0:
+                        quantise_v(rnd - 1)
+                    if rnd >= 1 and r == 1:
+                        attend(rnd - 1)
+                    b = PLAIN_BUNCHES + rnd * ROWS + r
+                    if b <= BUNCHES:
+                        attention_bunch(b)
+            quantise_v(ROUNDS - 1)
+            attend(ROUNDS - 1)

@@ -26,6 +26,7 @@ HEADS = 8
 DK = 128
 HALF = DK // 2
 SCALE = DK ** -0.5
+UNITS = HEADS * ROWS
 
 CHUNK_GROUPS = 2
 CHUNK_K = CHUNK_GROUPS * K_PASS
@@ -36,10 +37,10 @@ ROUND_HEADS = 2
 ROUND_COLS = ROUND_HEADS * DK
 ROUNDS = HEADS // ROUND_HEADS
 
-BUNCH = 2
-BUNCHES = HEADS * ROWS // BUNCH
-HEAD_BUNCHES = ROWS // BUNCH
-PLAIN_BUNCHES = 6
+SLOT = 2
+E_LAG = 3
+SLOTS = (UNITS + E_LAG) // SLOT + 1
+EARLY_SLOTS = 3
 
 TWO_PI_PARTS = (6.28125, 0.0019353071693331003, 1.0253131677018246e-11)
 SIN_BOUND = 3.1415925
@@ -60,18 +61,16 @@ def tile_multiheadedattention_pb_k_kernel(tc, q_rot, k_rot, values, wv_words, wv
     with ExitStack() as ctx:
         ctx.enter_context(tc.manual_schedule())
         keep = ctx.enter_context(tc.tile_pool(name="keep", bufs=1))
-        e_pool = ctx.enter_context(tc.tile_pool(name="e_pool", bufs=2 * BUNCH))
+        qk_pool = ctx.enter_context(tc.tile_pool(name="qk_pool", bufs=2))
+        e_pool = ctx.enter_context(tc.tile_pool(name="e_pool", bufs=E_LAG + SLOT + 1))
         eg_pool = ctx.enter_context(tc.tile_pool(name="eg_pool", bufs=2))
-        small = ctx.enter_context(tc.tile_pool(name="small", bufs=2 * BUNCH))
-        ps_sc = ctx.enter_context(tc.psum_pool(name="ps_sc", bufs=BUNCH))
-        ps_tp = ctx.enter_context(tc.psum_pool(name="ps_tp", bufs=2))
+        small = ctx.enter_context(tc.tile_pool(name="small", bufs=4))
 
         ident_bf = keep.tile([P, P], BF16)
         ident_f32 = keep.tile([P, P], F32)
         x_codes = keep.tile([P, GROUPS, SEQ], U32, align_bytes=64)
         x_scales = keep.tile([P, GROUPS, SEQ], U8, align_bytes=64)
         w_planes = keep.tile([P, GROUPS // 4, WIDTH], U8, align_bytes=64)
-        qk_raw = keep.tile([P, 2, HEADS, SEQ], BF16)
         qk_t = keep.tile([P, HEADS, 2 * ROWS, P], BF16)
         e_codes = keep.tile([P, HEADS, SEQ], U32, align_bytes=64)
         e_scales = keep.tile([P, HEADS, SEQ], U8, align_bytes=64)
@@ -86,70 +85,78 @@ def tile_multiheadedattention_pb_k_kernel(tc, q_rot, k_rot, values, wv_words, wv
             keep.tile([P, GROUPS, ROUND_COLS], U32, align_bytes=64, name="w_codes_%d" % rnd) for rnd in range(2)
         ]
 
+        pools = {}
+        qk_tiles = {}
         e_tiles = {}
         e_groups = {}
+        v_rows = {}
+        y_tiles = {}
 
         def load_qk(pair):
             heads = slice(2 * pair, 2 * pair + 2)
-            nc.sync.dma_start(out=qk_raw[:, 1, heads, :], in_=k_view[:, heads, :])
-            nc.sync.dma_start(out=qk_raw[:, 0, heads, :], in_=q_view[:, heads, :])
+            qk_raw = qk_pool.tile([P, 2, 2, SEQ], BF16, tag="qk_raw")
+            nc.sync.dma_start(out=qk_raw[:, 1, :, :], in_=k_view[:, heads, :])
+            nc.sync.dma_start(out=qk_raw[:, 0, :, :], in_=q_view[:, heads, :])
+            qk_tiles[pair] = qk_raw
 
-        def load_w(rnd, tile_):
+        def load_w(rnd, gs):
             cols = slice(rnd * ROUND_COLS, (rnd + 1) * ROUND_COLS)
-            for half in range(2):
-                gs = slice(half * GROUPS // 2, (half + 1) * GROUPS // 2)
-                nc.sync.dma_start(out=tile_[:, gs, :].bitcast(I32), in_=w_view[:, gs, cols])
+            nc.sync.dma_start(out=w_codes[rnd][:, gs, :].bitcast(I32), in_=w_view[:, gs, cols])
+
+        def load_scales(a):
+            for quad in range(4):
+                nc.sync.dma_start(
+                    out=w_planes[32 * quad : 32 * quad + 16, a, :].bitcast(I32),
+                    in_=s_view[4 * a : 4 * a + 4, 4 * quad : 4 * quad + 4, :],
+                )
 
         def transpose_qk(h):
-            tp = ps_tp.tile([P, 2 * ROWS, P], BF16, tag="tp")
+            tp = pools["tp"].tile([P, 2 * ROWS, P], BF16, tag="tp")
             for which in range(2):
                 for row in range(ROWS):
                     nc.tensor.transpose(
-                        tp[:, which * ROWS + row, :], qk_raw[:, which, h, row * DK : (row + 1) * DK], ident_bf[:]
+                        tp[:, which * ROWS + row, :],
+                        qk_tiles[h // 2][:, which, h % 2, row * DK : (row + 1) * DK],
+                        ident_bf[:],
                     )
             nc.scalar.copy(out=qk_t[:, h, :, :], in_=tp[:])
+            if h % 2 == 1 and h // 2 + 2 < HEADS // 2:
+                load_qk(h // 2 + 2)
 
-        def scores(b):
-            h = b // HEAD_BUNCHES
-            e_tiles[b] = []
-            for i in range(BUNCH):
-                a = (b % HEAD_BUNCHES) * BUNCH + i
-                sc = ps_sc.tile([P, SEQ], F32, tag="sc")
-                nc.tensor.matmul(
-                    out=sc[:],
-                    lhsT=qk_t[:, h, a, :],
-                    rhs=qk_t[:, h, ROWS : 2 * ROWS, :].rearrange("d r s -> d (r s)"),
-                    start=True,
-                    stop=True,
-                )
-                top = small.tile([P, 1], F32, tag="top")
-                nc.vector.reduce_max(out=top[:], in_=sc[:], axis=AX.X)
-                shift = small.tile([P, 1], F32, tag="shift")
-                nc.vector.tensor_scalar_mul(out=shift[:], in0=top[:], scalar1=-SCALE)
-                e_sb = e_pool.tile([P, SEQ], BF16, tag="e_sb")
-                nc.scalar.activation(
-                    out=e_sb[:],
-                    in_=sc[:],
-                    func=ACT.Exp,
-                    bias=shift[:],
-                    scale=SCALE,
-                    accum_out=rowsum[:, a, h : h + 1],
-                )
-                e_tiles[b].append(e_sb)
-
-        def transpose_e(b):
-            h = b // HEAD_BUNCHES
-            first = (b % HEAD_BUNCHES) * BUNCH
-            if first == 0:
-                e_groups[h] = eg_pool.tile([P, ROWS, P, PACK], BF16, align_bytes=64, tag="e_grp", name="e_grp")
-            tp = ps_tp.tile([P, BUNCH * ROWS, P], BF16, tag="tp")
-            for i in range(BUNCH):
-                for r in range(ROWS):
-                    nc.tensor.transpose(tp[:, i * ROWS + r, :], e_tiles[b][i][:, r * P : (r + 1) * P], ident_bf[:])
-            nc.scalar.copy(
-                out=e_groups[h][:, first : first + BUNCH, :, :],
-                in_=tp[:].rearrange("p (a r) t -> p a t r", r=ROWS),
+        def scores(unit):
+            h = unit // ROWS
+            a = unit % ROWS
+            sc = pools["sc"].tile([P, SEQ], F32, tag="sc")
+            nc.tensor.matmul(
+                out=sc[:],
+                lhsT=qk_t[:, h, a, :],
+                rhs=qk_t[:, h, ROWS : 2 * ROWS, :].rearrange("d r s -> d (r s)"),
+                start=True,
+                stop=True,
             )
+            top = small.tile([P, 1], F32, tag="top")
+            nc.vector.reduce_max(out=top[:], in_=sc[:], axis=AX.X)
+            shift = small.tile([P, 1], F32, tag="shift")
+            nc.vector.tensor_scalar_mul(out=shift[:], in0=top[:], scalar1=-SCALE)
+            e_sb = e_pool.tile([P, SEQ], BF16, tag="e_sb")
+            nc.scalar.activation(
+                out=e_sb[:], in_=sc[:], func=ACT.Exp, bias=shift[:], scale=SCALE, accum_out=rowsum[:, a, h : h + 1]
+            )
+            e_tiles[unit] = e_sb
+
+        def transpose_e(units):
+            tp = pools["tp"].tile([P, SLOT * ROWS, P], BF16, tag="tp")
+            for i, unit in enumerate(units):
+                for r in range(ROWS):
+                    nc.tensor.transpose(tp[:, i * ROWS + r, :], e_tiles[unit][:, r * P : (r + 1) * P], ident_bf[:])
+            for i, unit in enumerate(units):
+                h = unit // ROWS
+                a = unit % ROWS
+                if a == 0:
+                    e_groups[h] = eg_pool.tile([P, ROWS, P, PACK], BF16, align_bytes=64, tag="e_grp", name="e_grp")
+                nc.scalar.copy(
+                    out=e_groups[h][:, a, :, :], in_=tp[:, i * ROWS : (i + 1) * ROWS, :].rearrange("p r t -> p t r")
+                )
 
         def quantise_e(h):
             nc.vector.quantize_mx(
@@ -158,49 +165,145 @@ def tile_multiheadedattention_pb_k_kernel(tc, q_rot, k_rot, values, wv_words, wv
                 in_=e_groups[h][:].rearrange("p a t r -> p (a t r)"),
             )
 
-        def attention_bunch(b):
-            if b >= 1:
-                transpose_e(b - 1)
-            if b % HEAD_BUNCHES == HEAD_BUNCHES - 1 and b + 1 < BUNCHES:
-                transpose_qk((b + 1) // HEAD_BUNCHES)
-            if b < BUNCHES:
-                scores(b)
-            if b >= 1 and b % HEAD_BUNCHES == 0:
-                quantise_e(b // HEAD_BUNCHES - 1)
+        def attention_slot(slot):
+            first = slot * SLOT
+            done = [unit for unit in (first - E_LAG, first - E_LAG + 1) if 0 <= unit < UNITS]
+            if done:
+                transpose_e(done)
+            if (first + SLOT) % ROWS == 0 and first + SLOT < UNITS:
+                transpose_qk((first + SLOT) // ROWS)
+            for unit in range(first, min(first + SLOT, UNITS)):
+                scores(unit)
+            for unit in done:
+                if unit % ROWS == ROWS - 1:
+                    quantise_e(unit // ROWS)
 
-        with ExitStack() as plain:
-            x_pool = plain.enter_context(tc.tile_pool(name="x_pool", bufs=X_BUFS))
-            grp_pool = plain.enter_context(tc.tile_pool(name="grp_pool", bufs=3))
-            tab = plain.enter_context(tc.tile_pool(name="tab", bufs=1))
-            ps_xt = plain.enter_context(tc.psum_pool(name="ps_xt", bufs=4))
+        def project(rnd, r, z, groups):
+            rows = slice(r * P, (r + 1) * P)
+            cols = slice(rnd * ROUND_COLS, (rnd + 1) * ROUND_COLS)
+            for g in groups:
+                nc.tensor.matmul_mx(
+                    out=z[:],
+                    lhsT=x_codes[:, g, rows].bitcast(FP8X4),
+                    lhsT_scale=x_scales[:, g, rows],
+                    rhs=w_codes[rnd][:, g, :].bitcast(FP8X4),
+                    rhs_scale=w_planes[4 * (g % 4) : P, g // 4, cols],
+                    start=(g == 0),
+                    stop=(g == GROUPS - 1),
+                )
+
+        def rotate(rnd, r, z):
+            if r == 0:
+                v_rows[rnd] = pools["v"].tile([P, ROWS, 2, ROUND_COLS // 2], BF16, tag="v_rows", name="v_rows")
+            eng = nc.vector if rnd == ROUNDS - 1 else nc.gpsimd
+            xs = slice(rnd * ROUND_COLS // 2, (rnd + 1) * ROUND_COLS // 2)
+            zb = pools["rope"].tile([P, 2, ROUND_COLS // 2], F32, tag="zb")
+            nc.vector.tensor_tensor(
+                out=zb[:], in0=z[:].rearrange("p (x two) -> p two x", two=2), in1=bias_pl[:, :, xs], op=ALU.add
+            )
+            by_cos = pools["rope"].tile([P, 2, ROUND_COLS // 2], F32, tag="by_cos")
+            by_sin = pools["rope"].tile([P, 2, ROUND_COLS // 2], F32, tag="by_sin")
+            for table, prod in ((cos_t, by_cos), (sin_t, by_sin)):
+                eng.tensor_tensor(
+                    out=prod[:].rearrange("p two (h i) -> p (two h) i", i=HALF),
+                    in0=zb[:].rearrange("p two (h i) -> p (two h) i", i=HALF),
+                    in1=table[:, r, :].unsqueeze(1).to_broadcast([P, 2 * ROUND_HEADS, HALF]),
+                    op=ALU.mult,
+                )
+            eng.tensor_tensor(out=v_rows[rnd][:, r, 0, :], in0=by_cos[:, 0, :], in1=by_sin[:, 1, :], op=ALU.subtract)
+            eng.tensor_tensor(out=v_rows[rnd][:, r, 1, :], in0=by_cos[:, 1, :], in1=by_sin[:, 0, :], op=ALU.add)
+
+        def quantise_v(rnd):
+            cols = slice(rnd * ROUND_COLS, (rnd + 1) * ROUND_COLS)
+            v_grp = pools["v"].tile([P, ROUND_COLS, PACK], BF16, align_bytes=64, tag="v_grp")
+            nc.vector.tensor_copy(
+                out=v_grp[:].rearrange("p (x two) r -> p x two r", two=2),
+                in_=v_rows[rnd][:].rearrange("p r two x -> p x two r"),
+            )
+            nc.vector.quantize_mx(
+                out=v_codes[:, cols].bitcast(FP8X4),
+                scales=v_scales[:, cols],
+                in_=v_grp[:].rearrange("p n r -> p (n r)"),
+            )
+
+        def attend(rnd, pair):
+            heads = slice(rnd * ROUND_HEADS, (rnd + 1) * ROUND_HEADS)
+            rows = slice(2 * pair, 2 * pair + 2)
+            if pair == 0:
+                nc.vector.reciprocal(out=rinv[:, :, heads], in_=rowsum[:, :, heads])
+                y_tiles[rnd] = pools["v"].tile([P, ROWS, ROUND_COLS], F32, tag="y_sb", name="y_sb")
+            y = pools["sc"].tile([P, 2, ROUND_HEADS, DK], F32, tag="sc")
+            for a2 in range(2):
+                a = 2 * pair + a2
+                for h2 in range(ROUND_HEADS):
+                    h = rnd * ROUND_HEADS + h2
+                    nc.tensor.matmul_mx(
+                        out=y[:, a2, h2, :],
+                        lhsT=e_codes[:, h, a * P : (a + 1) * P].bitcast(FP8X4),
+                        lhsT_scale=e_scales[:, h, a * P : (a + 1) * P],
+                        rhs=v_codes[:, h * DK : (h + 1) * DK].bitcast(FP8X4),
+                        rhs_scale=v_scales[:, h * DK : (h + 1) * DK],
+                        start=True,
+                        stop=True,
+                    )
+            nc.vector.tensor_tensor(
+                out=y_tiles[rnd][:, rows, :].rearrange("p a (h j) -> p a h j", j=DK),
+                in0=y[:],
+                in1=rinv[:, rows, heads].unsqueeze(3).to_broadcast([P, 2, ROUND_HEADS, DK]),
+                op=ALU.mult,
+            )
+            nc.sync.dma_start(
+                out=out_view[:, rows, rnd * ROUND_COLS : (rnd + 1) * ROUND_COLS], in_=y_tiles[rnd][:, rows, :]
+            )
+
+        with ExitStack() as phase_1:
+            x_pool = phase_1.enter_context(tc.tile_pool(name="x_pool", bufs=X_BUFS))
+            grp_pool = phase_1.enter_context(tc.tile_pool(name="grp_pool", bufs=3))
+            tab = phase_1.enter_context(tc.tile_pool(name="tab", bufs=1))
+            ps_xt = phase_1.enter_context(tc.psum_pool(name="ps_xt", bufs=4))
+            pools["sc"] = phase_1.enter_context(tc.psum_pool(name="ps_sc_1", bufs=2))
+            pools["tp"] = phase_1.enter_context(tc.psum_pool(name="ps_tp_1", bufs=2))
+
+            x_tiles = []
+            b_raw = tab.tile([P, WIDTH], BF16)
 
             def load_chunk(c):
                 x_raw = x_pool.tile([P, ROWS, CHUNK_K], BF16, tag="x_raw")
                 nc.sync.dma_start(out=x_raw[:], in_=x_view[:, :, c * CHUNK_K : (c + 1) * CHUNK_K])
-                return x_raw
+                x_tiles.append(x_raw)
 
-            x_tiles = []
-            load_qk(0)
-            for c in range(4):
-                x_tiles.append(load_chunk(c))
-            load_qk(1)
-            for c in range(4, X_BUFS):
-                x_tiles.append(load_chunk(c))
+            def load_rest():
+                for a in range(GROUPS // 4):
+                    load_scales(a)
+                for rnd in range(2):
+                    for half in range(2):
+                        load_w(rnd, slice(half * GROUPS // 2, (half + 1) * GROUPS // 2))
+                    if rnd == 0:
+                        load_qk(1)
+                nc.sync.dma_start(out=b_raw[:], in_=bv.partition_broadcast(P))
+                nc.gpsimd.tensor_copy(out=bias_pl[:], in_=b_raw[:].rearrange("p (x two) -> p two x", two=2))
 
-            make_identity(nc, ident_bf[:])
-            make_identity(nc, ident_f32[:])
             nc.vector.memset(w_planes[:].bitcast(I32), 0)
+            load_qk(0)
+            for c in range(X_BUFS):
+                load_chunk(c)
 
             idx_i = tab.tile([P, HALF], I32)
             nc.gpsimd.iota(idx_i[:], pattern=[[1, HALF]], base=0, channel_multiplier=0)
             pos_i = tab.tile([P, ROWS], I32)
             nc.gpsimd.iota(pos_i[:], pattern=[[1, ROWS]], base=0, channel_multiplier=ROWS)
+            make_identity(nc, ident_bf[:])
+            make_identity(nc, ident_f32[:])
+            zero = tab.tile([P, 1], F32)
+            nc.vector.memset(zero[:], 0.0)
             idx_f = tab.tile([P, HALF], F32)
             nc.vector.tensor_copy(out=idx_f[:], in_=idx_i[:])
             pos_f = tab.tile([P, ROWS], F32)
             nc.vector.tensor_copy(out=pos_f[:], in_=pos_i[:])
             freq = tab.tile([P, HALF], F32)
             nc.scalar.activation(out=freq[:], in_=idx_f[:], func=ACT.Exp, scale=-2.0 * math.log(10000.0) / DK)
+            warm = tab.tile([P, 1], F32)
+            nc.scalar.activation(out=warm[:], in_=zero[:], func=ACT.Sin)
             angle = tab.tile([P, ROWS, HALF], F32)
             nc.vector.tensor_tensor(
                 out=angle[:],
@@ -227,27 +330,13 @@ def tile_multiheadedattention_pb_k_kernel(tc, q_rot, k_rot, values, wv_words, wv
             nc.vector.tensor_scalar(
                 out=angle[:], in0=angle[:], scalar1=-SIN_BOUND, scalar2=SIN_BOUND, op0=ALU.max, op1=ALU.min
             )
+            transpose_qk(0)
             nc.scalar.activation(out=sin_t[:], in_=angle[:], func=ACT.Sin)
             half_sin = tab.tile([P, ROWS, HALF], F32)
             nc.scalar.activation(out=half_sin[:], in_=angle[:], func=ACT.Sin, scale=0.5)
+            nc.scalar.activation(out=warm[:], in_=zero[:], func=ACT.Exp)
             nc.gpsimd.tensor_tensor(out=half_sin[:], in0=half_sin[:], in1=half_sin[:], op=ALU.mult)
             nc.gpsimd.tensor_scalar(out=cos_t[:], in0=half_sin[:], scalar1=-2.0, scalar2=1.0, op0=ALU.mult, op1=ALU.add)
-
-            b_raw = tab.tile([P, WIDTH], BF16)
-
-            def load_rest():
-                for a in range(GROUPS // 4):
-                    for quad in range(4):
-                        nc.sync.dma_start(
-                            out=w_planes[32 * quad : 32 * quad + 16, a, :].bitcast(I32),
-                            in_=s_view[4 * a : 4 * a + 4, 4 * quad : 4 * quad + 4, :],
-                        )
-                load_w(0, w_codes[0])
-                nc.sync.dma_start(out=b_raw[:], in_=bv.partition_broadcast(P))
-                nc.gpsimd.tensor_copy(out=bias_pl[:], in_=b_raw[:].rearrange("p (x two) -> p two x", two=2))
-                load_qk(2)
-                load_w(1, w_codes[1])
-                load_qk(3)
 
             def transpose_group(g):
                 x_raw = x_tiles[g // CHUNK_GROUPS]
@@ -274,122 +363,47 @@ def tile_multiheadedattention_pb_k_kernel(tc, q_rot, k_rot, values, wv_words, wv
                     in_=grouped[:].rearrange("p r s j -> p (r s j)"),
                 )
 
-            transpose_qk(0)
+            attention_slot(0)
             waiting = None
             for g in range(GROUPS):
                 grouped = transpose_group(g)
                 if waiting is not None:
                     quantise_group(g - 1, waiting)
                 waiting = grouped
-                next_chunk = g // CHUNK_GROUPS + X_BUFS
-                if g % CHUNK_GROUPS == CHUNK_GROUPS - 1 and next_chunk < CHUNKS:
-                    x_tiles.append(load_chunk(next_chunk))
-                    if next_chunk == CHUNKS - 1:
+                chunk = g // CHUNK_GROUPS + X_BUFS
+                if g % CHUNK_GROUPS == CHUNK_GROUPS - 1 and chunk < CHUNKS:
+                    load_chunk(chunk)
+                    if chunk == CHUNKS - 1:
                         load_rest()
-                for b in range(g * PLAIN_BUNCHES // GROUPS, (g + 1) * PLAIN_BUNCHES // GROUPS):
-                    attention_bunch(b)
             quantise_group(GROUPS - 1, waiting)
+            for slot in range(1, EARLY_SLOTS):
+                attention_slot(slot)
 
-        with ExitStack() as mx:
-            late = mx.enter_context(tc.tile_pool(name="late", bufs=1, reuse_waits="tile"))
-            rope = mx.enter_context(tc.tile_pool(name="rope", bufs=3, reuse_waits="tile"))
-            v_pool = mx.enter_context(tc.tile_pool(name="v_pool", bufs=2, reuse_waits="tile"))
-            ps_z = mx.enter_context(tc.psum_pool(name="ps_z", bufs=2, reuse_waits="tile"))
-            ps_y = mx.enter_context(tc.psum_pool(name="ps_y", bufs=2, reuse_waits="tile"))
+        with ExitStack() as phase_2:
+            late = phase_2.enter_context(tc.tile_pool(name="late", bufs=1, reuse_waits="tile"))
+            pools["rope"] = phase_2.enter_context(tc.tile_pool(name="rope", bufs=3, reuse_waits="tile"))
+            pools["v"] = phase_2.enter_context(tc.tile_pool(name="v_pool", bufs=2, reuse_waits="tile"))
+            ps_z = phase_2.enter_context(tc.psum_pool(name="ps_z", bufs=2, reuse_waits="tile"))
+            pools["sc"] = phase_2.enter_context(tc.psum_pool(name="ps_sc_2", bufs=4, reuse_waits="tile"))
+            pools["tp"] = phase_2.enter_context(tc.psum_pool(name="ps_tp_2", bufs=2, reuse_waits="tile"))
 
             for rnd in range(2, ROUNDS):
                 w_codes.append(late.tile([P, GROUPS, ROUND_COLS], U32, align_bytes=64, name="w_codes_%d" % rnd))
-                load_w(rnd, w_codes[rnd])
-
-            v_rows = {}
-
-            def project(rnd, r):
-                z = ps_z.tile([P, ROUND_COLS], F32, tag="z")
-                rows = slice(r * P, (r + 1) * P)
-                cols = slice(rnd * ROUND_COLS, (rnd + 1) * ROUND_COLS)
-                for g in range(GROUPS):
-                    nc.tensor.matmul_mx(
-                        out=z[:],
-                        lhsT=x_codes[:, g, rows].bitcast(FP8X4),
-                        lhsT_scale=x_scales[:, g, rows],
-                        rhs=w_codes[rnd][:, g, :].bitcast(FP8X4),
-                        rhs_scale=w_planes[4 * (g % 4) : P, g // 4, cols],
-                        start=(g == 0),
-                        stop=(g == GROUPS - 1),
-                    )
-                return z
-
-            def rotate(rnd, r, z):
-                if r == 0:
-                    v_rows[rnd] = v_pool.tile([P, ROWS, 2, ROUND_COLS // 2], BF16, tag="v_rows", name="v_rows")
-                eng = nc.vector if rnd == ROUNDS - 1 else nc.gpsimd
-                xs = slice(rnd * ROUND_COLS // 2, (rnd + 1) * ROUND_COLS // 2)
-                zb = rope.tile([P, 2, ROUND_COLS // 2], F32, tag="zb")
-                nc.vector.tensor_tensor(
-                    out=zb[:], in0=z[:].rearrange("p (x two) -> p two x", two=2), in1=bias_pl[:, :, xs], op=ALU.add
-                )
-                by_cos = rope.tile([P, 2, ROUND_COLS // 2], F32, tag="by_cos")
-                by_sin = rope.tile([P, 2, ROUND_COLS // 2], F32, tag="by_sin")
-                for table, prod in ((cos_t, by_cos), (sin_t, by_sin)):
-                    eng.tensor_tensor(
-                        out=prod[:].rearrange("p two (h i) -> p (two h) i", i=HALF),
-                        in0=zb[:].rearrange("p two (h i) -> p (two h) i", i=HALF),
-                        in1=table[:, r, :].unsqueeze(1).to_broadcast([P, 2 * ROUND_HEADS, HALF]),
-                        op=ALU.mult,
-                    )
-                eng.tensor_tensor(out=v_rows[rnd][:, r, 0, :], in0=by_cos[:, 0, :], in1=by_sin[:, 1, :], op=ALU.subtract)
-                eng.tensor_tensor(out=v_rows[rnd][:, r, 1, :], in0=by_cos[:, 1, :], in1=by_sin[:, 0, :], op=ALU.add)
-
-            def quantise_v(rnd):
-                cols = slice(rnd * ROUND_COLS, (rnd + 1) * ROUND_COLS)
-                v_grp = v_pool.tile([P, ROUND_COLS, PACK], BF16, align_bytes=64, tag="v_grp")
-                nc.vector.tensor_copy(
-                    out=v_grp[:].rearrange("p (x two) r -> p x two r", two=2),
-                    in_=v_rows[rnd][:].rearrange("p r two x -> p x two r"),
-                )
-                nc.vector.quantize_mx(
-                    out=v_codes[:, cols].bitcast(FP8X4),
-                    scales=v_scales[:, cols],
-                    in_=v_grp[:].rearrange("p n r -> p (n r)"),
-                )
-
-            def attend(rnd):
-                heads = slice(rnd * ROUND_HEADS, (rnd + 1) * ROUND_HEADS)
-                nc.vector.reciprocal(out=rinv[:, :, heads], in_=rowsum[:, :, heads])
-                y_sb = v_pool.tile([P, ROWS, ROUND_COLS], F32, tag="y_sb")
-                for pair in range(ROWS // 2):
-                    y = ps_y.tile([P, 2, ROUND_HEADS, DK], F32, tag="y")
-                    for a2 in range(2):
-                        a = 2 * pair + a2
-                        for h2 in range(ROUND_HEADS):
-                            h = rnd * ROUND_HEADS + h2
-                            nc.tensor.matmul_mx(
-                                out=y[:, a2, h2, :],
-                                lhsT=e_codes[:, h, a * P : (a + 1) * P].bitcast(FP8X4),
-                                lhsT_scale=e_scales[:, h, a * P : (a + 1) * P],
-                                rhs=v_codes[:, h * DK : (h + 1) * DK].bitcast(FP8X4),
-                                rhs_scale=v_scales[:, h * DK : (h + 1) * DK],
-                                start=True,
-                                stop=True,
-                            )
-                    nc.vector.tensor_tensor(
-                        out=y_sb[:, 2 * pair : 2 * pair + 2, :].rearrange("p a (h j) -> p a h j", j=DK),
-                        in0=y[:],
-                        in1=rinv[:, 2 * pair : 2 * pair + 2, heads].unsqueeze(3).to_broadcast([P, 2, ROUND_HEADS, DK]),
-                        op=ALU.mult,
-                    )
-                nc.sync.dma_start(out=out_view[:, :, rnd * ROUND_COLS : (rnd + 1) * ROUND_COLS], in_=y_sb[:])
+                for half in range(2):
+                    load_w(rnd, slice(half * GROUPS // 2, (half + 1) * GROUPS // 2))
 
             for rnd in range(ROUNDS):
                 for r in range(ROWS):
-                    z = project(rnd, r)
+                    z = ps_z.tile([P, ROUND_COLS], F32, tag="z")
+                    project(rnd, r, z, range(GROUPS))
                     rotate(rnd, r, z)
                     if rnd >= 1 and r == 0:
                         quantise_v(rnd - 1)
-                    if rnd >= 1 and r == 1:
-                        attend(rnd - 1)
-                    b = PLAIN_BUNCHES + rnd * ROWS + r
-                    if b <= BUNCHES:
-                        attention_bunch(b)
+                    if rnd >= 1 and 1 <= r <= ROWS // 2:
+                        attend(rnd - 1, r - 1)
+                    slot = EARLY_SLOTS + rnd * ROWS + r
+                    if slot < SLOTS:
+                        attention_slot(slot)
             quantise_v(ROUNDS - 1)
-            attend(ROUNDS - 1)
+            for pair in range(ROWS // 2):
+                attend(ROUNDS - 1, pair)

@@ -27,20 +27,21 @@ DK = 128
 HALF = DK // 2
 SCALE = DK ** -0.5
 UNITS = HEADS * ROWS
+BANK = 512
 
-CHUNK_GROUPS = 2
-CHUNK_K = CHUNK_GROUPS * K_PASS
-CHUNKS = GROUPS // CHUNK_GROUPS
-X_BUFS = 6
+QUAD = 4
+QUADS = GROUPS // QUAD
+X_BUFS = 2 * QUADS
 
 ROUND_HEADS = 2
 ROUND_COLS = ROUND_HEADS * DK
 ROUNDS = HEADS // ROUND_HEADS
+W_BUFS = 3
 
 SLOT = 2
 E_LAG = 3
 SLOTS = (UNITS + E_LAG) // SLOT + 1
-EARLY_SLOTS = 3
+EARLY_SLOTS = SLOTS - ROUNDS * ROWS
 
 TWO_PI_PARTS = (6.28125, 0.0019353071693331003, 1.0253131677018246e-11)
 SIN_BOUND = 3.1415925
@@ -55,21 +56,27 @@ def tile_multiheadedattention_pb_k_kernel(tc, q_rot, k_rot, values, wv_words, wv
     q_view = q_rot.rearrange("o h (p a) d -> p (o h) (a d)", a=ROWS)
     k_view = k_rot.rearrange("o h (p r) d -> p (o h) (r d)", r=ROWS)
     w_view = wv_words.rearrange("g p n t -> p g (n t)").bitcast(I32)
-    s_view = wv_scales.bitcast(I32)
+    s_view = wv_scales.bitcast(F32)
     out_view = out.rearrange("o (p a) n -> (o p) a n", a=ROWS)
 
     with ExitStack() as ctx:
         ctx.enter_context(tc.manual_schedule())
         keep = ctx.enter_context(tc.tile_pool(name="keep", bufs=1))
+        w_pool = ctx.enter_context(tc.tile_pool(name="w_pool", bufs=W_BUFS))
         qk_pool = ctx.enter_context(tc.tile_pool(name="qk_pool", bufs=2))
+        x_pool = ctx.enter_context(tc.tile_pool(name="x_pool", bufs=X_BUFS))
+        grp_pool = ctx.enter_context(tc.tile_pool(name="grp_pool", bufs=3))
         e_pool = ctx.enter_context(tc.tile_pool(name="e_pool", bufs=E_LAG + SLOT + 1))
         eg_pool = ctx.enter_context(tc.tile_pool(name="eg_pool", bufs=2))
         small = ctx.enter_context(tc.tile_pool(name="small", bufs=4))
+        ps_bank = ctx.enter_context(tc.psum_pool(name="ps_bank", bufs=4))
+        ps_tp = ctx.enter_context(tc.psum_pool(name="ps_tp", bufs=2))
+        ps_z = ctx.enter_context(tc.psum_pool(name="ps_z", bufs=2))
 
         ident_bf = keep.tile([P, P], BF16)
         ident_f32 = keep.tile([P, P], F32)
-        x_codes = keep.tile([P, GROUPS, SEQ], U32, align_bytes=64)
-        x_scales = keep.tile([P, GROUPS, SEQ], U8, align_bytes=64)
+        x_codes = keep.tile([P, ROWS, GROUPS, P], U32, align_bytes=64)
+        x_scales = keep.tile([P, ROWS, GROUPS, P], U8, align_bytes=64)
         w_planes = keep.tile([P, GROUPS // 4, WIDTH], U8, align_bytes=64)
         qk_t = keep.tile([P, HEADS, 2 * ROWS, P], BF16)
         e_codes = keep.tile([P, HEADS, SEQ], U32, align_bytes=64)
@@ -81,12 +88,10 @@ def tile_multiheadedattention_pb_k_kernel(tc, q_rot, k_rot, values, wv_words, wv
         bias_pl = keep.tile([P, 2, WIDTH // 2], F32)
         rowsum = keep.tile([P, ROWS, HEADS], F32)
         rinv = keep.tile([P, ROWS, HEADS], F32)
-        w_codes = [
-            keep.tile([P, GROUPS, ROUND_COLS], U32, align_bytes=64, name="w_codes_%d" % rnd) for rnd in range(2)
-        ]
 
-        pools = {}
+        w_codes = {}
         qk_tiles = {}
+        x_tiles = {}
         e_tiles = {}
         e_groups = {}
         v_rows = {}
@@ -99,19 +104,30 @@ def tile_multiheadedattention_pb_k_kernel(tc, q_rot, k_rot, values, wv_words, wv
             nc.sync.dma_start(out=qk_raw[:, 0, :, :], in_=q_view[:, heads, :])
             qk_tiles[pair] = qk_raw
 
-        def load_w(rnd, gs):
+        def load_w(rnd):
             cols = slice(rnd * ROUND_COLS, (rnd + 1) * ROUND_COLS)
-            nc.sync.dma_start(out=w_codes[rnd][:, gs, :].bitcast(I32), in_=w_view[:, gs, cols])
+            words = w_pool.tile([P, GROUPS, ROUND_COLS], U32, align_bytes=64, tag="w_codes")
+            for half in range(2):
+                gs = slice(half * GROUPS // 2, (half + 1) * GROUPS // 2)
+                nc.sync.dma_start(out=words[:, gs, :].bitcast(I32), in_=w_view[:, gs, cols])
+            w_codes[rnd] = words
 
-        def load_scales(a):
-            for quad in range(4):
-                nc.sync.dma_start(
-                    out=w_planes[32 * quad : 32 * quad + 16, a, :].bitcast(I32),
-                    in_=s_view[4 * a : 4 * a + 4, 4 * quad : 4 * quad + 4, :],
-                )
+        def load_row(r):
+            for quad in range(QUADS):
+                x_raw = x_pool.tile([P, QUAD * K_PASS], BF16, tag="x_raw")
+                nc.sync.dma_start(out=x_raw[:], in_=x_view[:, r, quad * QUAD * K_PASS : (quad + 1) * QUAD * K_PASS])
+                x_tiles[(r, quad)] = x_raw
+
+        def load_scales():
+            for a in range(GROUPS // 4):
+                for quad in range(4):
+                    nc.gpsimd.dma_start(
+                        out=w_planes[32 * quad : 32 * quad + 16, a, :].bitcast(F32),
+                        in_=s_view[4 * a : 4 * a + 4, 4 * quad : 4 * quad + 4, :],
+                    )
 
         def transpose_qk(h):
-            tp = pools["tp"].tile([P, 2 * ROWS, P], BF16, tag="tp")
+            tp = ps_tp.tile([P, 2 * ROWS, P], BF16, tag="tp")
             for which in range(2):
                 for row in range(ROWS):
                     nc.tensor.transpose(
@@ -126,7 +142,7 @@ def tile_multiheadedattention_pb_k_kernel(tc, q_rot, k_rot, values, wv_words, wv
         def scores(unit):
             h = unit // ROWS
             a = unit % ROWS
-            sc = pools["sc"].tile([P, SEQ], F32, tag="sc")
+            sc = ps_bank.tile([P, BANK], F32, tag="bank")
             nc.tensor.matmul(
                 out=sc[:],
                 lhsT=qk_t[:, h, a, :],
@@ -145,7 +161,7 @@ def tile_multiheadedattention_pb_k_kernel(tc, q_rot, k_rot, values, wv_words, wv
             e_tiles[unit] = e_sb
 
         def transpose_e(units):
-            tp = pools["tp"].tile([P, SLOT * ROWS, P], BF16, tag="tp")
+            tp = ps_tp.tile([P, SLOT * ROWS, P], BF16, tag="tp")
             for i, unit in enumerate(units):
                 for r in range(ROWS):
                     nc.tensor.transpose(tp[:, i * ROWS + r, :], e_tiles[unit][:, r * P : (r + 1) * P], ident_bf[:])
@@ -178,115 +194,51 @@ def tile_multiheadedattention_pb_k_kernel(tc, q_rot, k_rot, values, wv_words, wv
                 if unit % ROWS == ROWS - 1:
                     quantise_e(unit // ROWS)
 
-        def project(rnd, r, z, groups):
-            rows = slice(r * P, (r + 1) * P)
-            cols = slice(rnd * ROUND_COLS, (rnd + 1) * ROUND_COLS)
-            for g in groups:
-                nc.tensor.matmul_mx(
-                    out=z[:],
-                    lhsT=x_codes[:, g, rows].bitcast(FP8X4),
-                    lhsT_scale=x_scales[:, g, rows],
-                    rhs=w_codes[rnd][:, g, :].bitcast(FP8X4),
-                    rhs_scale=w_planes[4 * (g % 4) : P, g // 4, cols],
-                    start=(g == 0),
-                    stop=(g == GROUPS - 1),
-                )
+        def transpose_quad(r, quad):
+            x_raw = x_tiles[(r, quad)]
+            grouped = grp_pool.tile([P, QUAD, P, PACK], BF16, align_bytes=64, tag="grouped")
+            for half in range(2):
+                xt = ps_bank.tile([P, 2, 2, P], F32, tag="bank")
+                for g2 in range(2):
+                    first_k = (2 * half + g2) * K_PASS
+                    words = x_raw[:, first_k : first_k + K_PASS].bitcast(F32)
+                    for u in range(2):
+                        nc.tensor.transpose(xt[:, g2, u, :], words[:, u : K_PASS // 2 : 2], ident_f32[:])
+                dst = grouped[:, 2 * half : 2 * half + 2, :, :].bitcast(F32)
+                src = xt[:].rearrange("p g u s -> p g s u")
+                if half == 0:
+                    nc.vector.tensor_copy(out=dst, in_=src)
+                else:
+                    nc.scalar.copy(out=dst, in_=src)
+            return grouped
 
-        def rotate(rnd, r, z):
-            if r == 0:
-                v_rows[rnd] = pools["v"].tile([P, ROWS, 2, ROUND_COLS // 2], BF16, tag="v_rows", name="v_rows")
-            eng = nc.vector if rnd == ROUNDS - 1 else nc.gpsimd
-            xs = slice(rnd * ROUND_COLS // 2, (rnd + 1) * ROUND_COLS // 2)
-            zb = pools["rope"].tile([P, 2, ROUND_COLS // 2], F32, tag="zb")
-            nc.vector.tensor_tensor(
-                out=zb[:], in0=z[:].rearrange("p (x two) -> p two x", two=2), in1=bias_pl[:, :, xs], op=ALU.add
-            )
-            by_cos = pools["rope"].tile([P, 2, ROUND_COLS // 2], F32, tag="by_cos")
-            by_sin = pools["rope"].tile([P, 2, ROUND_COLS // 2], F32, tag="by_sin")
-            for table, prod in ((cos_t, by_cos), (sin_t, by_sin)):
-                eng.tensor_tensor(
-                    out=prod[:].rearrange("p two (h i) -> p (two h) i", i=HALF),
-                    in0=zb[:].rearrange("p two (h i) -> p (two h) i", i=HALF),
-                    in1=table[:, r, :].unsqueeze(1).to_broadcast([P, 2 * ROUND_HEADS, HALF]),
-                    op=ALU.mult,
-                )
-            eng.tensor_tensor(out=v_rows[rnd][:, r, 0, :], in0=by_cos[:, 0, :], in1=by_sin[:, 1, :], op=ALU.subtract)
-            eng.tensor_tensor(out=v_rows[rnd][:, r, 1, :], in0=by_cos[:, 1, :], in1=by_sin[:, 0, :], op=ALU.add)
-
-        def quantise_v(rnd):
-            cols = slice(rnd * ROUND_COLS, (rnd + 1) * ROUND_COLS)
-            v_grp = pools["v"].tile([P, ROUND_COLS, PACK], BF16, align_bytes=64, tag="v_grp")
-            nc.vector.tensor_copy(
-                out=v_grp[:].rearrange("p (x two) r -> p x two r", two=2),
-                in_=v_rows[rnd][:].rearrange("p r two x -> p x two r"),
-            )
+        def quantise_quad(r, quad, grouped):
+            gs = slice(quad * QUAD, (quad + 1) * QUAD)
             nc.vector.quantize_mx(
-                out=v_codes[:, cols].bitcast(FP8X4),
-                scales=v_scales[:, cols],
-                in_=v_grp[:].rearrange("p n r -> p (n r)"),
+                out=x_codes[:, r, gs, :].rearrange("p g s -> p (g s)").bitcast(FP8X4),
+                scales=x_scales[:, r, gs, :].rearrange("p g s -> p (g s)"),
+                in_=grouped[:].rearrange("p g s j -> p (g s j)"),
             )
 
-        def attend(rnd, pair):
-            heads = slice(rnd * ROUND_HEADS, (rnd + 1) * ROUND_HEADS)
-            rows = slice(2 * pair, 2 * pair + 2)
-            if pair == 0:
-                nc.vector.reciprocal(out=rinv[:, :, heads], in_=rowsum[:, :, heads])
-                y_tiles[rnd] = pools["v"].tile([P, ROWS, ROUND_COLS], F32, tag="y_sb", name="y_sb")
-            y = pools["sc"].tile([P, 2, ROUND_HEADS, DK], F32, tag="sc")
-            for a2 in range(2):
-                a = 2 * pair + a2
-                for h2 in range(ROUND_HEADS):
-                    h = rnd * ROUND_HEADS + h2
-                    nc.tensor.matmul_mx(
-                        out=y[:, a2, h2, :],
-                        lhsT=e_codes[:, h, a * P : (a + 1) * P].bitcast(FP8X4),
-                        lhsT_scale=e_scales[:, h, a * P : (a + 1) * P],
-                        rhs=v_codes[:, h * DK : (h + 1) * DK].bitcast(FP8X4),
-                        rhs_scale=v_scales[:, h * DK : (h + 1) * DK],
-                        start=True,
-                        stop=True,
-                    )
-            nc.vector.tensor_tensor(
-                out=y_tiles[rnd][:, rows, :].rearrange("p a (h j) -> p a h j", j=DK),
-                in0=y[:],
-                in1=rinv[:, rows, heads].unsqueeze(3).to_broadcast([P, 2, ROUND_HEADS, DK]),
-                op=ALU.mult,
-            )
-            nc.sync.dma_start(
-                out=out_view[:, rows, rnd * ROUND_COLS : (rnd + 1) * ROUND_COLS], in_=y_tiles[rnd][:, rows, :]
-            )
+        def transpose_row(r):
+            waiting = None
+            for quad in range(QUADS):
+                grouped = transpose_quad(r, quad)
+                if waiting is not None:
+                    quantise_quad(r, quad - 1, waiting)
+                waiting = grouped
+            quantise_quad(r, QUADS - 1, waiting)
 
-        with ExitStack() as phase_1:
-            x_pool = phase_1.enter_context(tc.tile_pool(name="x_pool", bufs=X_BUFS))
-            grp_pool = phase_1.enter_context(tc.tile_pool(name="grp_pool", bufs=3))
-            tab = phase_1.enter_context(tc.tile_pool(name="tab", bufs=1))
-            ps_xt = phase_1.enter_context(tc.psum_pool(name="ps_xt", bufs=4))
-            pools["sc"] = phase_1.enter_context(tc.psum_pool(name="ps_sc_1", bufs=2))
-            pools["tp"] = phase_1.enter_context(tc.psum_pool(name="ps_tp_1", bufs=2))
-
-            x_tiles = []
-            b_raw = tab.tile([P, WIDTH], BF16)
-
-            def load_chunk(c):
-                x_raw = x_pool.tile([P, ROWS, CHUNK_K], BF16, tag="x_raw")
-                nc.sync.dma_start(out=x_raw[:], in_=x_view[:, :, c * CHUNK_K : (c + 1) * CHUNK_K])
-                x_tiles.append(x_raw)
-
-            def load_rest():
-                for a in range(GROUPS // 4):
-                    load_scales(a)
-                for rnd in range(2):
-                    for half in range(2):
-                        load_w(rnd, slice(half * GROUPS // 2, (half + 1) * GROUPS // 2))
-                    if rnd == 0:
-                        load_qk(1)
-                nc.sync.dma_start(out=b_raw[:], in_=bv.partition_broadcast(P))
-                nc.gpsimd.tensor_copy(out=bias_pl[:], in_=b_raw[:].rearrange("p (x two) -> p two x", two=2))
-
+        with tc.tile_pool(name="tab", bufs=1) as tab:
             nc.vector.memset(w_planes[:].bitcast(I32), 0)
+            b_row = tab.tile([P, WIDTH], BF16)
+            nc.vector.memset(b_row[:].bitcast(I32), 0)
+            nc.sync.dma_start(out=b_row[0:1, :], in_=bv.rearrange("(o n) -> o n", o=1))
             load_qk(0)
-            for c in range(X_BUFS):
-                load_chunk(c)
+            load_row(0)
+            load_w(0)
+            load_row(1)
+            load_qk(1)
 
             idx_i = tab.tile([P, HALF], I32)
             nc.gpsimd.iota(idx_i[:], pattern=[[1, HALF]], base=0, channel_multiplier=0)
@@ -294,6 +246,9 @@ def tile_multiheadedattention_pb_k_kernel(tc, q_rot, k_rot, values, wv_words, wv
             nc.gpsimd.iota(pos_i[:], pattern=[[1, ROWS]], base=0, channel_multiplier=ROWS)
             make_identity(nc, ident_bf[:])
             make_identity(nc, ident_f32[:])
+            load_scales()
+            ones = tab.tile([P, P], BF16)
+            nc.vector.memset(ones[:], 1.0)
             zero = tab.tile([P, 1], F32)
             nc.vector.memset(zero[:], 0.0)
             idx_f = tab.tile([P, HALF], F32)
@@ -330,6 +285,19 @@ def tile_multiheadedattention_pb_k_kernel(tc, q_rot, k_rot, values, wv_words, wv
             nc.vector.tensor_scalar(
                 out=angle[:], in0=angle[:], scalar1=-SIN_BOUND, scalar2=SIN_BOUND, op0=ALU.max, op1=ALU.min
             )
+
+            for half in range(2):
+                spread = ps_bank.tile([P, BANK], F32, tag="bank")
+                nc.tensor.matmul(
+                    out=spread[:], lhsT=ones[:], rhs=b_row[:, half * BANK : (half + 1) * BANK], start=True, stop=True
+                )
+                dst = bias_pl[:, :, half * BANK // 2 : (half + 1) * BANK // 2]
+                src = spread[:].rearrange("p (x two) -> p two x", two=2)
+                if half == 0:
+                    nc.vector.tensor_copy(out=dst, in_=src)
+                else:
+                    nc.scalar.copy(out=dst, in_=src)
+
             transpose_qk(0)
             nc.scalar.activation(out=sin_t[:], in_=angle[:], func=ACT.Sin)
             half_sin = tab.tile([P, ROWS, HALF], F32)
@@ -338,72 +306,108 @@ def tile_multiheadedattention_pb_k_kernel(tc, q_rot, k_rot, values, wv_words, wv
             nc.gpsimd.tensor_tensor(out=half_sin[:], in0=half_sin[:], in1=half_sin[:], op=ALU.mult)
             nc.gpsimd.tensor_scalar(out=cos_t[:], in0=half_sin[:], scalar1=-2.0, scalar2=1.0, op0=ALU.mult, op1=ALU.add)
 
-            def transpose_group(g):
-                x_raw = x_tiles[g // CHUNK_GROUPS]
-                first_k = (g % CHUNK_GROUPS) * K_PASS
-                grouped = grp_pool.tile([P, ROWS, P, PACK], BF16, align_bytes=64, tag="grouped")
-                for half in range(2):
-                    xt = ps_xt.tile([P, 2, 2, P], F32, tag="xt")
-                    for r2 in range(2):
-                        words = x_raw[:, 2 * half + r2, first_k : first_k + K_PASS].bitcast(F32)
-                        for u in range(2):
-                            nc.tensor.transpose(xt[:, r2, u, :], words[:, u : K_PASS // 2 : 2], ident_f32[:])
-                    dst = grouped[:, 2 * half : 2 * half + 2, :, :].bitcast(F32)
-                    src = xt[:].rearrange("p r u s -> p r s u")
-                    if half == 0:
-                        nc.vector.tensor_copy(out=dst, in_=src)
-                    else:
-                        nc.scalar.copy(out=dst, in_=src)
-                return grouped
+        for slot in range(EARLY_SLOTS):
+            attention_slot(slot)
 
-            def quantise_group(g, grouped):
-                nc.vector.quantize_mx(
-                    out=x_codes[:, g, :].bitcast(FP8X4),
-                    scales=x_scales[:, g, :],
-                    in_=grouped[:].rearrange("p r s j -> p (r s j)"),
-                )
+        rope = ctx.enter_context(tc.tile_pool(name="rope", bufs=3, reuse_waits="tile"))
+        v_pool = ctx.enter_context(tc.tile_pool(name="v_pool", bufs=2, reuse_waits="tile"))
 
-            attention_slot(0)
-            waiting = None
+        def project(rnd, r):
+            z = ps_z.tile([P, ROUND_COLS], F32, tag="z")
+            cols = slice(rnd * ROUND_COLS, (rnd + 1) * ROUND_COLS)
             for g in range(GROUPS):
-                grouped = transpose_group(g)
-                if waiting is not None:
-                    quantise_group(g - 1, waiting)
-                waiting = grouped
-                chunk = g // CHUNK_GROUPS + X_BUFS
-                if g % CHUNK_GROUPS == CHUNK_GROUPS - 1 and chunk < CHUNKS:
-                    load_chunk(chunk)
-                    if chunk == CHUNKS - 1:
-                        load_rest()
-            quantise_group(GROUPS - 1, waiting)
-            for slot in range(1, EARLY_SLOTS):
-                attention_slot(slot)
+                nc.tensor.matmul_mx(
+                    out=z[:],
+                    lhsT=x_codes[:, r, g, :].bitcast(FP8X4),
+                    lhsT_scale=x_scales[:, r, g, :],
+                    rhs=w_codes[rnd][:, g, :].bitcast(FP8X4),
+                    rhs_scale=w_planes[4 * (g % 4) : P, g // 4, cols],
+                    start=(g == 0),
+                    stop=(g == GROUPS - 1),
+                )
+            return z
 
-        with ExitStack() as phase_2:
-            late = phase_2.enter_context(tc.tile_pool(name="late", bufs=1, reuse_waits="tile"))
-            pools["rope"] = phase_2.enter_context(tc.tile_pool(name="rope", bufs=3, reuse_waits="tile"))
-            pools["v"] = phase_2.enter_context(tc.tile_pool(name="v_pool", bufs=2, reuse_waits="tile"))
-            ps_z = phase_2.enter_context(tc.psum_pool(name="ps_z", bufs=2, reuse_waits="tile"))
-            pools["sc"] = phase_2.enter_context(tc.psum_pool(name="ps_sc_2", bufs=4, reuse_waits="tile"))
-            pools["tp"] = phase_2.enter_context(tc.psum_pool(name="ps_tp_2", bufs=2, reuse_waits="tile"))
+        def rotate(rnd, r, z):
+            if r == 0:
+                v_rows[rnd] = v_pool.tile([P, ROWS, 2, ROUND_COLS // 2], BF16, tag="v_rows", name="v_rows")
+            eng = nc.vector if rnd == ROUNDS - 1 else nc.gpsimd
+            xs = slice(rnd * ROUND_COLS // 2, (rnd + 1) * ROUND_COLS // 2)
+            zb = rope.tile([P, 2, ROUND_COLS // 2], F32, tag="zb")
+            nc.vector.tensor_tensor(
+                out=zb[:], in0=z[:].rearrange("p (x two) -> p two x", two=2), in1=bias_pl[:, :, xs], op=ALU.add
+            )
+            by_cos = rope.tile([P, 2, ROUND_COLS // 2], F32, tag="by_cos")
+            by_sin = rope.tile([P, 2, ROUND_COLS // 2], F32, tag="by_sin")
+            for table, prod in ((cos_t, by_cos), (sin_t, by_sin)):
+                eng.tensor_tensor(
+                    out=prod[:].rearrange("p two (h i) -> p (two h) i", i=HALF),
+                    in0=zb[:].rearrange("p two (h i) -> p (two h) i", i=HALF),
+                    in1=table[:, r, :].unsqueeze(1).to_broadcast([P, 2 * ROUND_HEADS, HALF]),
+                    op=ALU.mult,
+                )
+            eng.tensor_tensor(out=v_rows[rnd][:, r, 0, :], in0=by_cos[:, 0, :], in1=by_sin[:, 1, :], op=ALU.subtract)
+            eng.tensor_tensor(out=v_rows[rnd][:, r, 1, :], in0=by_cos[:, 1, :], in1=by_sin[:, 0, :], op=ALU.add)
 
-            for rnd in range(2, ROUNDS):
-                w_codes.append(late.tile([P, GROUPS, ROUND_COLS], U32, align_bytes=64, name="w_codes_%d" % rnd))
-                for half in range(2):
-                    load_w(rnd, slice(half * GROUPS // 2, (half + 1) * GROUPS // 2))
+        def quantise_v(rnd):
+            cols = slice(rnd * ROUND_COLS, (rnd + 1) * ROUND_COLS)
+            v_grp = v_pool.tile([P, ROUND_COLS, PACK], BF16, align_bytes=64, tag="v_grp")
+            nc.vector.tensor_copy(
+                out=v_grp[:].rearrange("p (x two) r -> p x two r", two=2),
+                in_=v_rows[rnd][:].rearrange("p r two x -> p x two r"),
+            )
+            nc.vector.quantize_mx(
+                out=v_codes[:, cols].bitcast(FP8X4),
+                scales=v_scales[:, cols],
+                in_=v_grp[:].rearrange("p n r -> p (n r)"),
+            )
 
-            for rnd in range(ROUNDS):
-                for r in range(ROWS):
-                    z = ps_z.tile([P, ROUND_COLS], F32, tag="z")
-                    project(rnd, r, z, range(GROUPS))
-                    rotate(rnd, r, z)
-                    if rnd >= 1 and r == 0:
-                        quantise_v(rnd - 1)
-                    if rnd >= 1 and 1 <= r <= ROWS // 2:
-                        attend(rnd - 1, r - 1)
-                    slot = EARLY_SLOTS + rnd * ROWS + r
-                    if slot < SLOTS:
-                        attention_slot(slot)
-            quantise_v(ROUNDS - 1)
-            for pair in range(ROWS // 2):
-                attend(ROUNDS - 1, pair)
+        def attend(rnd, pair):
+            heads = slice(rnd * ROUND_HEADS, (rnd + 1) * ROUND_HEADS)
+            rows = slice(2 * pair, 2 * pair + 2)
+            if pair == 0:
+                nc.vector.reciprocal(out=rinv[:, :, heads], in_=rowsum[:, :, heads])
+                y_tiles[rnd] = v_pool.tile([P, ROWS, ROUND_COLS], F32, tag="y_sb", name="y_sb")
+            y = ps_bank.tile([P, 2, ROUND_HEADS, DK], F32, tag="bank")
+            for a2 in range(2):
+                a = 2 * pair + a2
+                for h2 in range(ROUND_HEADS):
+                    h = rnd * ROUND_HEADS + h2
+                    nc.tensor.matmul_mx(
+                        out=y[:, a2, h2, :],
+                        lhsT=e_codes[:, h, a * P : (a + 1) * P].bitcast(FP8X4),
+                        lhsT_scale=e_scales[:, h, a * P : (a + 1) * P],
+                        rhs=v_codes[:, h * DK : (h + 1) * DK].bitcast(FP8X4),
+                        rhs_scale=v_scales[:, h * DK : (h + 1) * DK],
+                        start=True,
+                        stop=True,
+                    )
+            nc.vector.tensor_tensor(
+                out=y_tiles[rnd][:, rows, :].rearrange("p a (h j) -> p a h j", j=DK),
+                in0=y[:],
+                in1=rinv[:, rows, heads].unsqueeze(3).to_broadcast([P, 2, ROUND_HEADS, DK]),
+                op=ALU.mult,
+            )
+            nc.sync.dma_start(
+                out=out_view[:, rows, rnd * ROUND_COLS : (rnd + 1) * ROUND_COLS], in_=y_tiles[rnd][:, rows, :]
+            )
+
+        for rnd in range(ROUNDS):
+            for r in range(ROWS):
+                if rnd == 0:
+                    transpose_row(r)
+                    if r + 2 < ROWS:
+                        load_row(r + 2)
+                    if 1 <= r < W_BUFS:
+                        load_w(r)
+                if rnd == 1 and r == 0:
+                    load_w(W_BUFS)
+                attention_slot(EARLY_SLOTS + rnd * ROWS + r)
+                if rnd >= 1 and r >= ROWS // 2:
+                    attend(rnd - 1, r - ROWS // 2)
+                z = project(rnd, r)
+                rotate(rnd, r, z)
+                if rnd >= 1 and r == 0:
+                    quantise_v(rnd - 1)
+        quantise_v(ROUNDS - 1)
+        for pair in range(ROWS // 2):
+            attend(ROUNDS - 1, pair)

@@ -330,7 +330,7 @@ def tile_multiheadedattention_pb_k_kernel(tc, q_rot, k_rot, values, wv_words, wv
         def rotate(rnd, r, z):
             if r == 0:
                 v_rows[rnd] = v_pool.tile([P, ROWS, 2, ROUND_COLS // 2], BF16, tag="v_rows", name="v_rows")
-            eng = nc.vector if rnd == ROUNDS - 1 else nc.gpsimd
+            eng = nc.vector
             xs = slice(rnd * ROUND_COLS // 2, (rnd + 1) * ROUND_COLS // 2)
             zb = rope.tile([P, 2, ROUND_COLS // 2], F32, tag="zb")
             nc.vector.tensor_tensor(

@@ -94,7 +94,7 @@ def tile_multiheadedattention_pb_k_kernel(tc, q_rot, k_rot, values, wv_words, wv
         x_tiles = {}
         e_tiles = {}
         e_groups = {}
-        v_rows = {}
+        v_groups = {}
         y_tiles = {}
 
         def load_qk(pair):
@@ -139,26 +139,37 @@ def tile_multiheadedattention_pb_k_kernel(tc, q_rot, k_rot, values, wv_words, wv
             if h % 2 == 1 and h // 2 + 2 < HEADS // 2:
                 load_qk(h // 2 + 2)
 
-        def scores(unit):
-            h = unit // ROWS
-            a = unit % ROWS
-            sc = ps_bank.tile([P, BANK], F32, tag="bank")
-            nc.tensor.matmul(
-                out=sc[:],
-                lhsT=qk_t[:, h, a, :],
-                rhs=qk_t[:, h, ROWS : 2 * ROWS, :].rearrange("d r s -> d (r s)"),
-                start=True,
-                stop=True,
-            )
-            top = small.tile([P, 1], F32, tag="top")
-            nc.vector.reduce_max(out=top[:], in_=sc[:], axis=AX.X)
-            shift = small.tile([P, 1], F32, tag="shift")
-            nc.vector.tensor_scalar_mul(out=shift[:], in0=top[:], scalar1=-SCALE)
-            e_sb = e_pool.tile([P, SEQ], BF16, tag="e_sb")
-            nc.scalar.activation(
-                out=e_sb[:], in_=sc[:], func=ACT.Exp, bias=shift[:], scale=SCALE, accum_out=rowsum[:, a, h : h + 1]
-            )
-            e_tiles[unit] = e_sb
+        def scores(units):
+            banks = []
+            tops = []
+            for unit in units:
+                h = unit // ROWS
+                sc = ps_bank.tile([P, BANK], F32, tag="bank")
+                nc.tensor.matmul(
+                    out=sc[:],
+                    lhsT=qk_t[:, h, unit % ROWS, :],
+                    rhs=qk_t[:, h, ROWS : 2 * ROWS, :].rearrange("d r s -> d (r s)"),
+                    start=True,
+                    stop=True,
+                )
+                banks.append(sc)
+            for sc in banks:
+                top = small.tile([P, 1], F32, tag="top")
+                nc.vector.reduce_max(out=top[:], in_=sc[:], axis=AX.X)
+                tops.append(top)
+            for unit, sc, top in zip(units, banks, tops):
+                shift = small.tile([P, 1], F32, tag="shift")
+                nc.vector.tensor_scalar_mul(out=shift[:], in0=top[:], scalar1=-SCALE)
+                e_sb = e_pool.tile([P, SEQ], BF16, tag="e_sb")
+                nc.scalar.activation(
+                    out=e_sb[:],
+                    in_=sc[:],
+                    func=ACT.Exp,
+                    bias=shift[:],
+                    scale=SCALE,
+                    accum_out=rowsum[:, unit % ROWS, unit // ROWS : unit // ROWS + 1],
+                )
+                e_tiles[unit] = e_sb
 
         def transpose_e(units):
             tp = ps_tp.tile([P, SLOT * ROWS, P], BF16, tag="tp")
@@ -188,8 +199,8 @@ def tile_multiheadedattention_pb_k_kernel(tc, q_rot, k_rot, values, wv_words, wv
                 transpose_e(done)
             if (first + SLOT) % ROWS == 0 and first + SLOT < UNITS:
                 transpose_qk((first + SLOT) // ROWS)
-            for unit in range(first, min(first + SLOT, UNITS)):
-                scores(unit)
+            if first < UNITS:
+                scores(range(first, first + SLOT))
             for unit in done:
                 if unit % ROWS == ROWS - 1:
                     quantise_e(unit // ROWS)
@@ -329,8 +340,7 @@ def tile_multiheadedattention_pb_k_kernel(tc, q_rot, k_rot, values, wv_words, wv
 
         def rotate(rnd, r, z):
             if r == 0:
-                v_rows[rnd] = v_pool.tile([P, ROWS, 2, ROUND_COLS // 2], BF16, tag="v_rows", name="v_rows")
-            eng = nc.vector
+                v_groups[rnd] = v_pool.tile([P, ROUND_COLS, PACK], BF16, align_bytes=64, tag="v_grp", name="v_grp")
             xs = slice(rnd * ROUND_COLS // 2, (rnd + 1) * ROUND_COLS // 2)
             zb = rope.tile([P, 2, ROUND_COLS // 2], F32, tag="zb")
             nc.vector.tensor_tensor(
@@ -339,26 +349,22 @@ def tile_multiheadedattention_pb_k_kernel(tc, q_rot, k_rot, values, wv_words, wv
             by_cos = rope.tile([P, 2, ROUND_COLS // 2], F32, tag="by_cos")
             by_sin = rope.tile([P, 2, ROUND_COLS // 2], F32, tag="by_sin")
             for table, prod in ((cos_t, by_cos), (sin_t, by_sin)):
-                eng.tensor_tensor(
+                nc.gpsimd.tensor_tensor(
                     out=prod[:].rearrange("p two (h i) -> p (two h) i", i=HALF),
                     in0=zb[:].rearrange("p two (h i) -> p (two h) i", i=HALF),
                     in1=table[:, r, :].unsqueeze(1).to_broadcast([P, 2 * ROUND_HEADS, HALF]),
                     op=ALU.mult,
                 )
-            eng.tensor_tensor(out=v_rows[rnd][:, r, 0, :], in0=by_cos[:, 0, :], in1=by_sin[:, 1, :], op=ALU.subtract)
-            eng.tensor_tensor(out=v_rows[rnd][:, r, 1, :], in0=by_cos[:, 1, :], in1=by_sin[:, 0, :], op=ALU.add)
+            v_out = v_groups[rnd][:].rearrange("p (x two) r -> p two r x", two=2)
+            nc.gpsimd.tensor_tensor(out=v_out[:, 0, r, :], in0=by_cos[:, 0, :], in1=by_sin[:, 1, :], op=ALU.subtract)
+            nc.gpsimd.tensor_tensor(out=v_out[:, 1, r, :], in0=by_cos[:, 1, :], in1=by_sin[:, 0, :], op=ALU.add)
 
         def quantise_v(rnd):
             cols = slice(rnd * ROUND_COLS, (rnd + 1) * ROUND_COLS)
-            v_grp = v_pool.tile([P, ROUND_COLS, PACK], BF16, align_bytes=64, tag="v_grp")
-            nc.vector.tensor_copy(
-                out=v_grp[:].rearrange("p (x two) r -> p x two r", two=2),
-                in_=v_rows[rnd][:].rearrange("p r two x -> p x two r"),
-            )
             nc.vector.quantize_mx(
                 out=v_codes[:, cols].bitcast(FP8X4),
                 scales=v_scales[:, cols],
-                in_=v_grp[:].rearrange("p n r -> p (n r)"),
+                in_=v_groups[rnd][:].rearrange("p n r -> p (n r)"),
             )
 
         def attend(rnd, pair):
@@ -406,7 +412,7 @@ def tile_multiheadedattention_pb_k_kernel(tc, q_rot, k_rot, values, wv_words, wv
                     attend(rnd - 1, r - ROWS // 2)
                 z = project(rnd, r)
                 rotate(rnd, r, z)
-                if rnd >= 1 and r == 0:
+                if rnd >= 1 and r == 1:
                     quantise_v(rnd - 1)
         quantise_v(ROUNDS - 1)
         for pair in range(ROWS // 2):

import math
from contextlib import ExitStack

import concourse.mybir as mybir
from concourse.masks import make_identity

F32 = mybir.dt.float32
BF16 = mybir.dt.bfloat16
I32 = mybir.dt.int32
U32 = mybir.dt.uint32
U8 = mybir.dt.uint8
FP8X4 = mybir.dt.float8_e4m3fn_x4
ALU = mybir.AluOpType
ACT = mybir.ActivationFunctionType
AX = mybir.AxisListType

P = 128
PACK = 4
K_PASS = P * PACK
SEQ = 512
ROWS = SEQ // P
EMB = 8192
GROUPS = EMB // K_PASS
WIDTH = 1024
HEADS = 8
DK = 128
HALF = DK // 2
SCALE = DK ** -0.5
UNITS = HEADS * ROWS
BANK = 512

QUAD = 4
QUADS = GROUPS // QUAD
X_BUFS = 2 * QUADS

ROUND_HEADS = 2
ROUND_COLS = ROUND_HEADS * DK
ROUNDS = HEADS // ROUND_HEADS
W_BUFS = 3

SLOT = 2
E_LAG = 3
SLOTS = (UNITS + E_LAG) // SLOT + 1
EARLY_SLOTS = SLOTS - ROUNDS * ROWS

TWO_PI_PARTS = (6.28125, 0.0019353071693331003, 1.0253131677018246e-11)
SIN_BOUND = 3.1415925

FLOPS = 2 * SEQ * EMB * WIDTH + 2 * 2 * HEADS * SEQ * SEQ * DK


def tile_multiheadedattention_pb_k_kernel(tc, q_rot, k_rot, values, wv_words, wv_scales, bv, out):
    nc = tc.nc

    x_view = values.rearrange("o (p r) k -> (o p) r k", r=ROWS)
    q_view = q_rot.rearrange("o h (p a) d -> p (o h) (a d)", a=ROWS)
    k_view = k_rot.rearrange("o h (p r) d -> p (o h) (r d)", r=ROWS)
    w_view = wv_words.rearrange("g p n t -> p g (n t)").bitcast(I32)
    s_view = wv_scales.bitcast(F32)
    out_view = out.rearrange("o (p a) n -> (o p) a n", a=ROWS)

    with ExitStack() as ctx:
        ctx.enter_context(tc.manual_schedule())
        keep = ctx.enter_context(tc.tile_pool(name="keep", bufs=1))
        w_pool = ctx.enter_context(tc.tile_pool(name="w_pool", bufs=W_BUFS))
        qk_pool = ctx.enter_context(tc.tile_pool(name="qk_pool", bufs=2))
        x_pool = ctx.enter_context(tc.tile_pool(name="x_pool", bufs=X_BUFS))
        grp_pool = ctx.enter_context(tc.tile_pool(name="grp_pool", bufs=3))
        e_pool = ctx.enter_context(tc.tile_pool(name="e_pool", bufs=E_LAG + SLOT + 1))
        eg_pool = ctx.enter_context(tc.tile_pool(name="eg_pool", bufs=2))
        small = ctx.enter_context(tc.tile_pool(name="small", bufs=4))
        ps_bank = ctx.enter_context(tc.psum_pool(name="ps_bank", bufs=4))
        ps_tp = ctx.enter_context(tc.psum_pool(name="ps_tp", bufs=2))
        ps_z = ctx.enter_context(tc.psum_pool(name="ps_z", bufs=2))

        ident_bf = keep.tile([P, P], BF16)
        ident_f32 = keep.tile([P, P], F32)
        x_codes = keep.tile([P, ROWS, GROUPS, P], U32, align_bytes=64)
        x_scales = keep.tile([P, ROWS, GROUPS, P], U8, align_bytes=64)
        w_planes = keep.tile([P, GROUPS // 4, WIDTH], U8, align_bytes=64)
        qk_t = keep.tile([P, HEADS, 2 * ROWS, P], BF16)
        e_codes = keep.tile([P, HEADS, SEQ], U32, align_bytes=64)
        e_scales = keep.tile([P, HEADS, SEQ], U8, align_bytes=64)
        v_codes = keep.tile([P, WIDTH], U32, align_bytes=64)
        v_scales = keep.tile([P, WIDTH], U8, align_bytes=64)
        sin_t = keep.tile([P, ROWS, HALF], F32)
        cos_t = keep.tile([P, ROWS, HALF], F32)
        bias_pl = keep.tile([P, 2, WIDTH // 2], F32)
        rowsum = keep.tile([P, ROWS, HEADS], F32)
        rinv = keep.tile([P, ROWS, HEADS], F32)

        w_codes = {}
        qk_tiles = {}
        x_tiles = {}
        e_tiles = {}
        e_groups = {}
        v_groups = {}
        y_tiles = {}

        def load_qk(pair):
            heads = slice(2 * pair, 2 * pair + 2)
            qk_raw = qk_pool.tile([P, 2, 2, SEQ], BF16, tag="qk_raw")
            nc.sync.dma_start(out=qk_raw[:, 1, :, :], in_=k_view[:, heads, :])
            nc.sync.dma_start(out=qk_raw[:, 0, :, :], in_=q_view[:, heads, :])
            qk_tiles[pair] = qk_raw

        def load_w(rnd):
            cols = slice(rnd * ROUND_COLS, (rnd + 1) * ROUND_COLS)
            words = w_pool.tile([P, GROUPS, ROUND_COLS], U32, align_bytes=64, tag="w_codes")
            for half in range(2):
                gs = slice(half * GROUPS // 2, (half + 1) * GROUPS // 2)
                nc.sync.dma_start(out=words[:, gs, :].bitcast(I32), in_=w_view[:, gs, cols])
            w_codes[rnd] = words

        def load_row(r):
            for quad in range(QUADS):
                x_raw = x_pool.tile([P, QUAD * K_PASS], BF16, tag="x_raw")
                nc.sync.dma_start(out=x_raw[:], in_=x_view[:, r, quad * QUAD * K_PASS : (quad + 1) * QUAD * K_PASS])
                x_tiles[(r, quad)] = x_raw

        def load_scales():
            for a in range(GROUPS // 4):
                for quad in range(4):
                    nc.gpsimd.dma_start(
                        out=w_planes[32 * quad : 32 * quad + 16, a, :].bitcast(F32),
                        in_=s_view[4 * a : 4 * a + 4, 4 * quad : 4 * quad + 4, :],
                    )

        def transpose_qk(h):
            tp = ps_tp.tile([P, 2 * ROWS, P], BF16, tag="tp")
            for which in range(2):
                for row in range(ROWS):
                    nc.tensor.transpose(
                        tp[:, which * ROWS + row, :],
                        qk_tiles[h // 2][:, which, h % 2, row * DK : (row + 1) * DK],
                        ident_bf[:],
                    )
            nc.scalar.copy(out=qk_t[:, h, :, :], in_=tp[:])
            if h % 2 == 1 and h // 2 + 2 < HEADS // 2:
                load_qk(h // 2 + 2)

        def scores(units):
            banks = []
            tops = []
            for unit in units:
                h = unit // ROWS
                sc = ps_bank.tile([P, BANK], F32, tag="bank")
                nc.tensor.matmul(
                    out=sc[:],
                    lhsT=qk_t[:, h, unit % ROWS, :],
                    rhs=qk_t[:, h, ROWS : 2 * ROWS, :].rearrange("d r s -> d (r s)"),
                    start=True,
                    stop=True,
                )
                banks.append(sc)
            for sc in banks:
                top = small.tile([P, 1], F32, tag="top")
                nc.vector.reduce_max(out=top[:], in_=sc[:], axis=AX.X)
                tops.append(top)
            for unit, sc, top in zip(units, banks, tops):
                shift = small.tile([P, 1], F32, tag="shift")
                nc.vector.tensor_scalar_mul(out=shift[:], in0=top[:], scalar1=-SCALE)
                e_sb = e_pool.tile([P, SEQ], BF16, tag="e_sb")
                nc.scalar.activation(
                    out=e_sb[:],
                    in_=sc[:],
                    func=ACT.Exp,
                    bias=shift[:],
                    scale=SCALE,
                    accum_out=rowsum[:, unit % ROWS, unit // ROWS : unit // ROWS + 1],
                )
                e_tiles[unit] = e_sb

        def transpose_e(units):
            tp = ps_tp.tile([P, SLOT * ROWS, P], BF16, tag="tp")
            for i, unit in enumerate(units):
                for r in range(ROWS):
                    nc.tensor.transpose(tp[:, i * ROWS + r, :], e_tiles[unit][:, r * P : (r + 1) * P], ident_bf[:])
            for i, unit in enumerate(units):
                h = unit // ROWS
                a = unit % ROWS
                if a == 0:
                    e_groups[h] = eg_pool.tile([P, ROWS, P, PACK], BF16, align_bytes=64, tag="e_grp", name="e_grp")
                nc.scalar.copy(
                    out=e_groups[h][:, a, :, :], in_=tp[:, i * ROWS : (i + 1) * ROWS, :].rearrange("p r t -> p t r")
                )

        def quantise_e(h):
            nc.vector.quantize_mx(
                out=e_codes[:, h, :].bitcast(FP8X4),
                scales=e_scales[:, h, :],
                in_=e_groups[h][:].rearrange("p a t r -> p (a t r)"),
            )

        def attention_slot(slot):
            first = slot * SLOT
            done = [unit for unit in (first - E_LAG, first - E_LAG + 1) if 0 <= unit < UNITS]
            if done:
                transpose_e(done)
            if (first + SLOT) % ROWS == 0 and first + SLOT < UNITS:
                transpose_qk((first + SLOT) // ROWS)
            if first < UNITS:
                scores(range(first, first + SLOT))
            for unit in done:
                if unit % ROWS == ROWS - 1:
                    quantise_e(unit // ROWS)

        def transpose_quad(r, quad):
            x_raw = x_tiles[(r, quad)]
            grouped = grp_pool.tile([P, QUAD, P, PACK], BF16, align_bytes=64, tag="grouped")
            for half in range(2):
                xt = ps_bank.tile([P, 2, 2, P], F32, tag="bank")
                for g2 in range(2):
                    first_k = (2 * half + g2) * K_PASS
                    words = x_raw[:, first_k : first_k + K_PASS].bitcast(F32)
                    for u in range(2):
                        nc.tensor.transpose(xt[:, g2, u, :], words[:, u : K_PASS // 2 : 2], ident_f32[:])
                dst = grouped[:, 2 * half : 2 * half + 2, :, :].bitcast(F32)
                src = xt[:].rearrange("p g u s -> p g s u")
                if half == 0:
                    nc.vector.tensor_copy(out=dst, in_=src)
                else:
                    nc.scalar.copy(out=dst, in_=src)
            return grouped

        def quantise_quad(r, quad, grouped):
            gs = slice(quad * QUAD, (quad + 1) * QUAD)
            nc.vector.quantize_mx(
                out=x_codes[:, r, gs, :].rearrange("p g s -> p (g s)").bitcast(FP8X4),
                scales=x_scales[:, r, gs, :].rearrange("p g s -> p (g s)"),
                in_=grouped[:].rearrange("p g s j -> p (g s j)"),
            )

        def transpose_row(r):
            waiting = None
            for quad in range(QUADS):
                grouped = transpose_quad(r, quad)
                if waiting is not None:
                    quantise_quad(r, quad - 1, waiting)
                waiting = grouped
            quantise_quad(r, QUADS - 1, waiting)

        with tc.tile_pool(name="tab", bufs=1) as tab:
            nc.vector.memset(w_planes[:].bitcast(I32), 0)
            b_row = tab.tile([P, WIDTH], BF16)
            nc.vector.memset(b_row[:].bitcast(I32), 0)
            nc.sync.dma_start(out=b_row[0:1, :], in_=bv.rearrange("(o n) -> o n", o=1))
            load_qk(0)
            load_row(0)
            load_w(0)
            load_row(1)
            load_qk(1)

            idx_i = tab.tile([P, HALF], I32)
            nc.gpsimd.iota(idx_i[:], pattern=[[1, HALF]], base=0, channel_multiplier=0)
            pos_i = tab.tile([P, ROWS], I32)
            nc.gpsimd.iota(pos_i[:], pattern=[[1, ROWS]], base=0, channel_multiplier=ROWS)
            make_identity(nc, ident_bf[:])
            make_identity(nc, ident_f32[:])
            load_scales()
            ones = tab.tile([P, P], BF16)
            nc.vector.memset(ones[:], 1.0)
            zero = tab.tile([P, 1], F32)
            nc.vector.memset(zero[:], 0.0)
            idx_f = tab.tile([P, HALF], F32)
            nc.vector.tensor_copy(out=idx_f[:], in_=idx_i[:])
            pos_f = tab.tile([P, ROWS], F32)
            nc.vector.tensor_copy(out=pos_f[:], in_=pos_i[:])
            freq = tab.tile([P, HALF], F32)
            nc.scalar.activation(out=freq[:], in_=idx_f[:], func=ACT.Exp, scale=-2.0 * math.log(10000.0) / DK)
            warm = tab.tile([P, 1], F32)
            nc.scalar.activation(out=warm[:], in_=zero[:], func=ACT.Sin)
            angle = tab.tile([P, ROWS, HALF], F32)
            nc.vector.tensor_tensor(
                out=angle[:],
                in0=freq[:].unsqueeze(1).to_broadcast([P, ROWS, HALF]),
                in1=pos_f[:].unsqueeze(2).to_broadcast([P, ROWS, HALF]),
                op=ALU.mult,
            )
            turns_i = tab.tile([P, ROWS, HALF], I32)
            nc.vector.tensor_scalar_mul(out=turns_i[:], in0=angle[:], scalar1=0.5 / math.pi)
            cut = tab.tile([P, ROWS, HALF], F32)
            nc.vector.tensor_copy(out=cut[:], in_=turns_i[:])
            left = tab.tile([P, ROWS, HALF], F32)
            nc.vector.scalar_tensor_tensor(
                out=left[:], in0=cut[:], scalar=-2.0 * math.pi, in1=angle[:], op0=ALU.mult, op1=ALU.add
            )
            turns = tab.tile([P, ROWS, HALF], F32)
            nc.vector.scalar_tensor_tensor(
                out=turns[:], in0=left[:], scalar=math.pi, in1=cut[:], op0=ALU.is_gt, op1=ALU.add
            )
            for part in TWO_PI_PARTS:
                nc.vector.scalar_tensor_tensor(
                    out=angle[:], in0=turns[:], scalar=-part, in1=angle[:], op0=ALU.mult, op1=ALU.add
                )
            nc.vector.tensor_scalar(
                out=angle[:], in0=angle[:], scalar1=-SIN_BOUND, scalar2=SIN_BOUND, op0=ALU.max, op1=ALU.min
            )

            for half in range(2):
                spread = ps_bank.tile([P, BANK], F32, tag="bank")
                nc.tensor.matmul(
                    out=spread[:], lhsT=ones[:], rhs=b_row[:, half * BANK : (half + 1) * BANK], start=True, stop=True
                )
                dst = bias_pl[:, :, half * BANK // 2 : (half + 1) * BANK // 2]
                src = spread[:].rearrange("p (x two) -> p two x", two=2)
                if half == 0:
                    nc.vector.tensor_copy(out=dst, in_=src)
                else:
                    nc.scalar.copy(out=dst, in_=src)

            transpose_qk(0)
            nc.scalar.activation(out=sin_t[:], in_=angle[:], func=ACT.Sin)
            half_sin = tab.tile([P, ROWS, HALF], F32)
            nc.scalar.activation(out=half_sin[:], in_=angle[:], func=ACT.Sin, scale=0.5)
            nc.scalar.activation(out=warm[:], in_=zero[:], func=ACT.Exp)
            nc.gpsimd.tensor_tensor(out=half_sin[:], in0=half_sin[:], in1=half_sin[:], op=ALU.mult)
            nc.gpsimd.tensor_scalar(out=cos_t[:], in0=half_sin[:], scalar1=-2.0, scalar2=1.0, op0=ALU.mult, op1=ALU.add)

        for slot in range(EARLY_SLOTS):
            attention_slot(slot)

        rope = ctx.enter_context(tc.tile_pool(name="rope", bufs=3, reuse_waits="tile"))
        v_pool = ctx.enter_context(tc.tile_pool(name="v_pool", bufs=2, reuse_waits="tile"))

        def project(rnd, r):
            z = ps_z.tile([P, ROUND_COLS], F32, tag="z")
            cols = slice(rnd * ROUND_COLS, (rnd + 1) * ROUND_COLS)
            for g in range(GROUPS):
                nc.tensor.matmul_mx(
                    out=z[:],
                    lhsT=x_codes[:, r, g, :].bitcast(FP8X4),
                    lhsT_scale=x_scales[:, r, g, :],
                    rhs=w_codes[rnd][:, g, :].bitcast(FP8X4),
                    rhs_scale=w_planes[4 * (g % 4) : P, g // 4, cols],
                    start=(g == 0),
                    stop=(g == GROUPS - 1),
                )
            return z

        def rotate(rnd, r, z):
            if r == 0:
                v_groups[rnd] = v_pool.tile([P, ROUND_COLS, PACK], BF16, align_bytes=64, tag="v_grp", name="v_grp")
            xs = slice(rnd * ROUND_COLS // 2, (rnd + 1) * ROUND_COLS // 2)
            zb = rope.tile([P, 2, ROUND_COLS // 2], F32, tag="zb")
            nc.vector.tensor_tensor(
                out=zb[:], in0=z[:].rearrange("p (x two) -> p two x", two=2), in1=bias_pl[:, :, xs], op=ALU.add
            )
            by_cos = rope.tile([P, 2, ROUND_COLS // 2], F32, tag="by_cos")
            by_sin = rope.tile([P, 2, ROUND_COLS // 2], F32, tag="by_sin")
            for table, prod in ((cos_t, by_cos), (sin_t, by_sin)):
                nc.gpsimd.tensor_tensor(
                    out=prod[:].rearrange("p two (h i) -> p (two h) i", i=HALF),
                    in0=zb[:].rearrange("p two (h i) -> p (two h) i", i=HALF),
                    in1=table[:, r, :].unsqueeze(1).to_broadcast([P, 2 * ROUND_HEADS, HALF]),
                    op=ALU.mult,
                )
            v_out = v_groups[rnd][:].rearrange("p (x two) r -> p two r x", two=2)
            nc.gpsimd.tensor_tensor(out=v_out[:, 0, r, :], in0=by_cos[:, 0, :], in1=by_sin[:, 1, :], op=ALU.subtract)
            nc.gpsimd.tensor_tensor(out=v_out[:, 1, r, :], in0=by_cos[:, 1, :], in1=by_sin[:, 0, :], op=ALU.add)

        def quantise_v(rnd):
            cols = slice(rnd * ROUND_COLS, (rnd + 1) * ROUND_COLS)
            nc.vector.quantize_mx(
                out=v_codes[:, cols].bitcast(FP8X4),
                scales=v_scales[:, cols],
                in_=v_groups[rnd][:].rearrange("p n r -> p (n r)"),
            )

        def attend(rnd, pair):
            heads = slice(rnd * ROUND_HEADS, (rnd + 1) * ROUND_HEADS)
            rows = slice(2 * pair, 2 * pair + 2)
            if pair == 0:
                nc.vector.reciprocal(out=rinv[:, :, heads], in_=rowsum[:, :, heads])
                y_tiles[rnd] = v_pool.tile([P, ROWS, ROUND_COLS], F32, tag="y_sb", name="y_sb")
            y = ps_bank.tile([P, 2, ROUND_HEADS, DK], F32, tag="bank")
            for a2 in range(2):
                a = 2 * pair + a2
                for h2 in range(ROUND_HEADS):
                    h = rnd * ROUND_HEADS + h2
                    nc.tensor.matmul_mx(
                        out=y[:, a2, h2, :],
                        lhsT=e_codes[:, h, a * P : (a + 1) * P].bitcast(FP8X4),
                        lhsT_scale=e_scales[:, h, a * P : (a + 1) * P],
                        rhs=v_codes[:, h * DK : (h + 1) * DK].bitcast(FP8X4),
                        rhs_scale=v_scales[:, h * DK : (h + 1) * DK],
                        start=True,
                        stop=True,
                    )
            nc.vector.tensor_tensor(
                out=y_tiles[rnd][:, rows, :].rearrange("p a (h j) -> p a h j", j=DK),
                in0=y[:],
                in1=rinv[:, rows, heads].unsqueeze(3).to_broadcast([P, 2, ROUND_HEADS, DK]),
                op=ALU.mult,
            )
            nc.sync.dma_start(
                out=out_view[:, rows, rnd * ROUND_COLS : (rnd + 1) * ROUND_COLS], in_=y_tiles[rnd][:, rows, :]
            )

        for rnd in range(ROUNDS):
            for r in range(ROWS):
                if rnd == 0:
                    transpose_row(r)
                    if r + 2 < ROWS:
                        load_row(r + 2)
                    if 1 <= r < W_BUFS:
                        load_w(r)
                if rnd == 1 and r == 0:
                    load_w(W_BUFS)
                attention_slot(EARLY_SLOTS + rnd * ROWS + r)
                if rnd >= 1 and r >= ROWS // 2:
                    attend(rnd - 1, r - ROWS // 2)
                z = project(rnd, r)
                rotate(rnd, r, z)
                if rnd >= 1 and r == 1:
                    quantise_v(rnd - 1)
        quantise_v(ROUNDS - 1)
        for pair in range(ROWS // 2):
            attend(ROUNDS - 1, pair)
